import numpy as np
import ml_dtypes


def mxq(x, axis, fmt="e4m3"):
    dtype, down = {"e4m3": (ml_dtypes.float8_e4m3fn, 7), "e5m2": (ml_dtypes.float8_e5m2, 14)}[fmt]
    v = np.moveaxis(np.asarray(x, np.float32).astype(ml_dtypes.bfloat16).astype(np.float64), axis, -1)
    blocks = v.reshape(v.shape[:-1] + (-1, 32))
    amax = np.abs(blocks).max(-1, keepdims=True)
    byte = np.maximum(np.where(amax > 0, np.frexp(amax)[1] - 1 + 127, 0) - down, 1)
    scale = np.exp2(byte - 127.0)
    codes = (blocks / scale).astype(np.float32).astype(dtype).astype(np.float64)
    return np.moveaxis((codes * scale).reshape(v.shape), -1, axis)


WIDE = False


def mx_kscale(k):
    if not WIDE:
        return np.ones(k)
    levels = np.array([10, -10, 5, -5, 0])
    a = np.random.permutation(np.resize(levels, k // 512 * 4)).reshape(k // 512, 4)
    idx = np.arange(k)
    return np.exp2(a[idx // 512, idx % 128 // 32])


BF16 = ml_dtypes.bfloat16


def bf(x):
    return np.asarray(x, np.float32).astype(BF16)


def f64(x):
    return np.asarray(x).astype(np.float64)


B, D, F0, F1, F2, F3, P = 128, 1024, 512, 512, 256, 128, 200


def relu(v):
    return np.maximum(v, 0.0)


def neg_l1(feat, pr):
    return -np.stack([np.abs(feat - row).sum(-1) for row in pr], axis=1)


def setup_inputs():
    s = mx_kscale(F1)
    t = mx_kscale(F0)
    return {
        "x": bf(np.random.standard_normal((B, D))),
        "aW": bf(np.random.standard_normal((D, D)) * 0.7 / np.sqrt(D)),
        "ab": bf(np.random.standard_normal(D) * 0.5),
        "h_up": bf(np.maximum(np.random.standard_normal((B, F1)), 0.0) * 1.4 * s),
        "h_skip": bf(np.maximum(np.random.standard_normal((B, F1)), 0.0) * 1.4 * s),
        "Wu2": bf(np.random.standard_normal((F0, F1)) / np.sqrt(F1) / s[None, :] * t[:, None]),
        "bu2": bf(np.random.standard_normal(F0) * 0.8 * t),
        "Wu3": bf(np.random.standard_normal((D, F0)) * 1.4 / np.sqrt(F0) / t[None, :]),
        "bu3": bf(np.random.standard_normal(D) * 0.8),
        "protos": bf(np.random.standard_normal((P, D))),
    }


def reference(x, aW, ab, h_up, h_skip, Wu2, bu2, Wu3, bu3, protos):
    xf = f64(x)
    z = f64(h_up) + f64(h_skip)
    u2 = relu((mxq(z, 1, "e4m3") @ mxq(f64(Wu2), 1, "e4m3").T) + f64(bu2))
    u3 = relu((mxq(u2, 1, "e4m3") @ mxq(f64(Wu3), 1, "e4m3").T) + f64(bu3))
    feat = xf + ((mxq(xf, 1, "e4m3") @ mxq(f64(aW), 1, "e4m3").T) + f64(ab)) + u3
    return neg_l1(feat, f64(protos))

@@ -1,0 +1,302 @@
+import concourse.mybir as mybir
+from concourse.masks import make_identity
+
+F32 = mybir.dt.float32
+BF16 = mybir.dt.bfloat16
+U32 = mybir.dt.uint32
+U8 = mybir.dt.uint8
+FP8X4 = mybir.dt.float8_e4m3fn_x4
+ALU = mybir.AluOpType
+ACT = mybir.ActivationFunctionType
+
+P = 128
+PACK = 4
+K_PASS = P * PACK
+
+B, D, F0, F1, N_PROTO = 128, 1024, 512, 512, 200
+D_CHUNKS = D // P
+F0_CHUNKS = F0 // P
+X_PASSES = D // K_PASS
+BANK_CHUNKS = 4
+
+AB_ROW, BU3_ROW, BU2_ROW = 72, 73, 74
+AB_COL, BU3_COL, BU2_COL = P + AB_ROW, P + BU3_ROW, P + BU2_ROW
+
+SCALAR_CHUNKS = 3
+
+FLOPS = 2 * B * (F1 * F0 + F0 * D + D * D) + 3 * B * N_PROTO * D
+
+
+def tile_prototypelearnerv4_pa_s_kernel(
+    tc, x, aW, ab, h_up, h_skip, Wu2, bu2, Wu3, bu3, protos, out
+):
+    nc = tc.nc
+
+    with (
+        tc.tile_pool(name="keep", bufs=1) as keep,
+        tc.tile_pool(name="stage", bufs=4) as stage,
+        tc.tile_pool(name="work", bufs=8) as work,
+    ):
+        ident_bf = keep.tile([P, P], BF16)
+        make_identity(nc, ident_bf[:])
+        ident_f32 = keep.tile([P, P], F32)
+        make_identity(nc, ident_f32[:])
+
+        h_up_sb = keep.tile([P, F1], BF16)
+        h_skip_sb = keep.tile([P, F1], BF16)
+        stack = keep.tile([P, 2, D], BF16)
+        wu2_sb = keep.tile([P, F0_CHUNKS, F1], BF16)
+        wu3_sb = keep.tile([P, D_CHUNKS, F0], BF16)
+        x_sb = keep.tile([P, D], BF16)
+        aw_sb = keep.tile([P, D_CHUNKS, D], BF16)
+
+        nc.vector.memset(stack[:, 1, :], 0.0)
+        nc.sync.dma_start(out=h_up_sb[:], in_=h_up)
+        nc.sync.dma_start(out=h_skip_sb[:], in_=h_skip)
+        nc.sync.dma_start(out=stack[BU2_ROW : BU2_ROW + 1, 1, 0:F0], in_=bu2.unsqueeze(0))
+        nc.sync.dma_start(out=stack[BU3_ROW : BU3_ROW + 1, 1, :], in_=bu3.unsqueeze(0))
+        nc.sync.dma_start(out=stack[AB_ROW : AB_ROW + 1, 1, :], in_=ab.unsqueeze(0))
+        nc.sync.dma_start(out=stack[0 : N_PROTO - P, 1, :], in_=protos[P:N_PROTO, :])
+        nc.sync.dma_start(out=wu2_sb[:], in_=Wu2.rearrange("(r p) k -> p r k", p=P))
+        nc.sync.dma_start(out=wu3_sb[:], in_=Wu3.rearrange("(r p) k -> p r k", p=P))
+        nc.sync.dma_start(out=x_sb[:], in_=x)
+        for c in range(0, D_CHUNKS, 2):
+            nc.sync.dma_start(
+                out=aw_sb[:, c : c + 2, :],
+                in_=aW[c * P : (c + 2) * P, :].rearrange("(r p) k -> p r k", p=P),
+            )
+        nc.sync.dma_start(out=stack[:, 0, :], in_=protos[0:P, :])
+
+        z_codes = keep.tile([P, B], U32, align_bytes=64)
+        z_scales = keep.tile([P, B], U8, align_bytes=64)
+        u2_codes = keep.tile([P, B], U32, align_bytes=64)
+        u2_scales = keep.tile([P, B], U8, align_bytes=64)
+        x_codes = keep.tile([P, X_PASSES, B], U32, align_bytes=64)
+        x_scales = keep.tile([P, X_PASSES, B], U8, align_bytes=64)
+        wu2_codes = keep.tile([P, F0_CHUNKS, P], U32, align_bytes=64)
+        wu2_scales = keep.tile([P, F0_CHUNKS, P], U8, align_bytes=64)
+        wu3_codes = keep.tile([P, D_CHUNKS, P], U32, align_bytes=64)
+        wu3_scales = keep.tile([P, D_CHUNKS, P], U8, align_bytes=64)
+        aw_codes = keep.tile([P, D_CHUNKS, X_PASSES, P], U32, align_bytes=64)
+        aw_scales = keep.tile([P, D_CHUNKS, X_PASSES, P], U8, align_bytes=64)
+
+        x_grouped = keep.tile([P, X_PASSES, B, PACK], BF16, align_bytes=64)
+
+        q_tab = keep.tile([P, D_CHUNKS, 2 * P], F32)
+        neg_half_q = keep.tile([P, D_CHUNKS, 2 * P], F32)
+        featT = keep.tile([P, D_CHUNKS, B], F32)
+
+        with (
+            tc.psum_pool(name="psum_t", bufs=3) as psum_t,
+            tc.psum_pool(name="psum_mx", bufs=1) as psum_mx,
+        ):
+
+            def transpose_four(src):
+                xt = psum_t.tile([P, PACK, P], BF16)
+                for t in range(PACK):
+                    nc.tensor.transpose(xt[:, t, :], src[:, t * P : (t + 1) * P], ident_bf[:])
+                return xt
+
+            def quantise(grouped, codes, scales):
+                nc.vector.quantize_mx(
+                    out=codes.bitcast(FP8X4),
+                    scales=scales,
+                    in_=grouped.rearrange("p r t -> p (r t)"),
+                )
+
+            def to_mx_operand(index, src, grouped, codes, scales):
+                xt = transpose_four(src)
+                permuted = xt[:].rearrange("p t r -> p r t")
+                if index % 3 == 2:
+                    nc.vector.tensor_copy(out=grouped, in_=permuted)
+                else:
+                    nc.scalar.copy(out=grouped, in_=permuted)
+                quantise(grouped, codes, scales)
+
+            def new_grouped():
+                grouped = stage.tile([P, P, PACK], BF16, align_bytes=64)
+                return grouped[:]
+
+            z_sb = keep.tile([P, F1], BF16)
+            nc.vector.tensor_tensor(out=z_sb[:], in0=h_up_sb[:], in1=h_skip_sb[:], op=ALU.add)
+            to_mx_operand(0, z_sb[:], new_grouped(), z_codes[:], z_scales[:])
+            for r in range(F0_CHUNKS):
+                to_mx_operand(
+                    r, wu2_sb[:, r, :], new_grouped(), wu2_codes[:, r, :], wu2_scales[:, r, :]
+                )
+
+            for half in range(2):
+                xt = transpose_four(stack[:, 1, half * K_PASS : (half + 1) * K_PASS])
+                nc.scalar.copy(
+                    out=q_tab[:, half * PACK : (half + 1) * PACK, P : 2 * P], in_=xt[:]
+                )
+
+            u2_ps = psum_mx.tile([P, F0_CHUNKS, B], F32)
+            for r in range(F0_CHUNKS):
+                nc.tensor.matmul_mx(
+                    out=u2_ps[:, r, :],
+                    lhsT=wu2_codes[:, r, :].bitcast(FP8X4),
+                    lhsT_scale=wu2_scales[:, r, :],
+                    rhs=z_codes[:].bitcast(FP8X4),
+                    rhs_scale=z_scales[:],
+                    start=True,
+                    stop=True,
+                )
+            u2_bf = keep.tile([P, F0_CHUNKS, B], BF16)
+            for r in range(F0_CHUNKS):
+                nc.scalar.activation(
+                    out=u2_bf[:, r, :],
+                    in_=u2_ps[:, r, :],
+                    func=ACT.Relu,
+                    bias=q_tab[:, r, BU2_COL : BU2_COL + 1],
+                    scale=1.0,
+                )
+            u2_grouped = new_grouped()
+            nc.vector.tensor_copy(out=u2_grouped, in_=u2_bf[:].rearrange("p t r -> p r t"))
+            quantise(u2_grouped, u2_codes[:], u2_scales[:])
+
+            for c in range(D_CHUNKS):
+                to_mx_operand(
+                    c, wu3_sb[:, c, :], new_grouped(), wu3_codes[:, c, :], wu3_scales[:, c, :]
+                )
+            for g in range(X_PASSES):
+                to_mx_operand(
+                    g,
+                    x_sb[:, g * K_PASS : (g + 1) * K_PASS],
+                    x_grouped[:, g, :, :],
+                    x_codes[:, g, :],
+                    x_scales[:, g, :],
+                )
+            u3_ps = [
+                psum_mx.tile([P, BANK_CHUNKS, B], F32, name="u3_ps%d" % bank) for bank in range(2)
+            ]
+            for c in range(D_CHUNKS):
+                nc.tensor.matmul_mx(
+                    out=u3_ps[c // BANK_CHUNKS][:, c % BANK_CHUNKS, :],
+                    lhsT=wu3_codes[:, c, :].bitcast(FP8X4),
+                    lhsT_scale=wu3_scales[:, c, :],
+                    rhs=u2_codes[:].bitcast(FP8X4),
+                    rhs_scale=u2_scales[:],
+                    start=True,
+                    stop=True,
+                )
+            u3_sb = keep.tile([P, D_CHUNKS, B], F32)
+            rest = keep.tile([P, D_CHUNKS, B], F32)
+            for c in range(D_CHUNKS):
+                nc.scalar.activation(
+                    out=u3_sb[:, c, :],
+                    in_=u3_ps[c // BANK_CHUNKS][:, c % BANK_CHUNKS, :],
+                    func=ACT.Relu,
+                    bias=q_tab[:, c, BU3_COL : BU3_COL + 1],
+                    scale=1.0,
+                )
+                nc.vector.scalar_tensor_tensor(
+                    out=rest[:, c, :],
+                    in0=x_grouped[:, c // PACK, :, c % PACK],
+                    scalar=q_tab[:, c, AB_COL : AB_COL + 1],
+                    in1=u3_sb[:, c, :],
+                    op0=ALU.add,
+                    op1=ALU.add,
+                )
+
+            for c in range(D_CHUNKS):
+                for g in range(X_PASSES):
+                    to_mx_operand(
+                        c * X_PASSES + g,
+                        aw_sb[:, c, g * K_PASS : (g + 1) * K_PASS],
+                        new_grouped(),
+                        aw_codes[:, c, g, :],
+                        aw_scales[:, c, g, :],
+                    )
+            for half in range(2):
+                xt = transpose_four(stack[:, 0, half * K_PASS : (half + 1) * K_PASS])
+                nc.scalar.copy(out=q_tab[:, half * PACK : (half + 1) * PACK, 0:P], in_=xt[:])
+            nc.vector.tensor_scalar(
+                out=neg_half_q[:], in0=q_tab[:], scalar1=-0.5, scalar2=None, op0=ALU.mult
+            )
+
+            ad_ps = [
+                psum_mx.tile([P, BANK_CHUNKS, B], F32, name="ad_ps%d" % bank) for bank in range(2)
+            ]
+            for c in range(D_CHUNKS):
+                for g in range(X_PASSES):
+                    nc.tensor.matmul_mx(
+                        out=ad_ps[c // BANK_CHUNKS][:, c % BANK_CHUNKS, :],
+                        lhsT=aw_codes[:, c, g, :].bitcast(FP8X4),
+                        lhsT_scale=aw_scales[:, c, g, :],
+                        rhs=x_codes[:, g, :].bitcast(FP8X4),
+                        rhs_scale=x_scales[:, g, :],
+                        start=(g == 0),
+                        stop=(g == X_PASSES - 1),
+                    )
+            for bank in range(2):
+                chunks = slice(bank * BANK_CHUNKS, (bank + 1) * BANK_CHUNKS)
+                nc.vector.tensor_tensor(
+                    out=featT[:, chunks, :], in0=ad_ps[bank][:], in1=rest[:, chunks, :], op=ALU.add
+                )
+
+        with tc.psum_pool(name="psum_acc", bufs=6) as psum_acc:
+
+            def add_transposed(acc_slot, tile_in, first, last):
+                nc.tensor.matmul(
+                    out=acc_slot,
+                    lhsT=tile_in,
+                    rhs=ident_f32[:],
+                    start=first,
+                    stop=last,
+                    is_transpose=True,
+                )
+
+            feat_sum = keep.tile([P, 1], F32)
+            acc = psum_acc.tile([P, BANK_CHUNKS, B], F32)
+            for c in range(SCALAR_CHUNKS, D_CHUNKS):
+                add_transposed(acc[:, 0, :], featT[:, c, :], c == SCALAR_CHUNKS, c == D_CHUNKS - 1)
+            nc.vector.tensor_reduce(
+                out=feat_sum[:], in_=acc[:, 0, :], axis=mybir.AxisListType.X, op=ALU.add
+            )
+
+            half_sums = keep.tile([P, N_PROTO], F32)
+            for first_proto in range(0, N_PROTO, BANK_CHUNKS):
+                acc = psum_acc.tile([P, BANK_CHUNKS, B], F32)
+                for slot in range(BANK_CHUNKS):
+                    proto = first_proto + slot
+                    for c in range(D_CHUNKS):
+                        if c < SCALAR_CHUNKS:
+                            half_abs = work.tile([P, B], F32)
+                            nc.scalar.activation(
+                                out=half_abs[:],
+                                in_=featT[:, c, :],
+                                func=ACT.Abs,
+                                bias=neg_half_q[:, c, proto : proto + 1],
+                                scale=0.5,
+                            )
+                            term = half_abs
+                        else:
+                            half_max = work.tile([P, B], F32)
+                            nc.vector.tensor_scalar(
+                                out=half_max[:],
+                                in0=featT[:, c, :],
+                                scalar1=q_tab[:, c, proto : proto + 1],
+                                scalar2=neg_half_q[:, c, proto : proto + 1],
+                                op0=ALU.max,
+                                op1=ALU.add,
+                            )
+                            term = half_max
+                        add_transposed(acc[:, slot, :], term[:], c == 0, c == D_CHUNKS - 1)
+                nc.vector.tensor_reduce(
+                    out=half_sums[:, first_proto : first_proto + BANK_CHUNKS],
+                    in_=acc[:],
+                    axis=mybir.AxisListType.X,
+                    op=ALU.add,
+                )
+
+            result = keep.tile([P, N_PROTO], F32)
+            nc.vector.tensor_scalar(
+                out=result[:],
+                in0=half_sums[:],
+                scalar1=-2.0,
+                scalar2=feat_sum[:, 0:1],
+                op0=ALU.mult,
+                op1=ALU.add,
+            )
+            nc.sync.dma_start(out=out, in_=result[:])

@@ -8,10 +8,12 @@ U8 = mybir.dt.uint8
 FP8X4 = mybir.dt.float8_e4m3fn_x4
 ALU = mybir.AluOpType
 ACT = mybir.ActivationFunctionType
+AXIS_X = mybir.AxisListType.X
 
 P = 128
 PACK = 4
 K_PASS = P * PACK
+PAIR = 2
 
 B, D, F0, F1, N_PROTO = 128, 1024, 512, 512, 200
 D_CHUNKS = D // P
@@ -22,9 +24,13 @@ BANK_CHUNKS = 4
 AB_ROW, BU3_ROW, BU2_ROW = 72, 73, 74
 AB_COL, BU3_COL, BU2_COL = P + AB_ROW, P + BU3_ROW, P + BU2_ROW
 
-SCALAR_CHUNKS = 3
+SCALAR_CHUNKS = 5
 
 FLOPS = 2 * B * (F1 * F0 + F0 * D + D * D) + 3 * B * N_PROTO * D
+
+
+def pair_rows(w):
+    return w.rearrange("(g m e) k -> m g (e k)", m=P, e=PAIR)
 
 
 def tile_prototypelearnerv4_pa_s_kernel(
@@ -35,12 +41,15 @@ def tile_prototypelearnerv4_pa_s_kernel(
     with (
         tc.tile_pool(name="keep", bufs=1) as keep,
         tc.tile_pool(name="stage", bufs=4) as stage,
-        tc.tile_pool(name="work", bufs=8) as work,
+        tc.tile_pool(name="abs_tiles", bufs=20) as abs_tiles,
+        tc.tile_pool(name="sum_tiles", bufs=12) as sum_tiles,
     ):
         ident_bf = keep.tile([P, P], BF16)
         make_identity(nc, ident_bf[:])
         ident_f32 = keep.tile([P, P], F32)
         make_identity(nc, ident_f32[:])
+        ones_f32 = keep.tile([P, P], F32)
+        nc.vector.memset(ones_f32[:], 1.0)
 
         h_up_sb = keep.tile([P, F1], BF16)
         h_skip_sb = keep.tile([P, F1], BF16)
@@ -57,13 +66,17 @@ def tile_prototypelearnerv4_pa_s_kernel(
         nc.sync.dma_start(out=stack[BU3_ROW : BU3_ROW + 1, 1, :], in_=bu3.unsqueeze(0))
         nc.sync.dma_start(out=stack[AB_ROW : AB_ROW + 1, 1, :], in_=ab.unsqueeze(0))
         nc.sync.dma_start(out=stack[0 : N_PROTO - P, 1, :], in_=protos[P:N_PROTO, :])
-        nc.sync.dma_start(out=wu2_sb[:], in_=Wu2.rearrange("(r p) k -> p r k", p=P))
-        nc.sync.dma_start(out=wu3_sb[:], in_=Wu3.rearrange("(r p) k -> p r k", p=P))
+        nc.sync.dma_start(
+            out=wu2_sb[:].rearrange("m (g e) k -> m g (e k)", e=PAIR), in_=pair_rows(Wu2)
+        )
+        nc.sync.dma_start(
+            out=wu3_sb[:].rearrange("m (g e) k -> m g (e k)", e=PAIR), in_=pair_rows(Wu3)
+        )
         nc.sync.dma_start(out=x_sb[:], in_=x)
-        for c in range(0, D_CHUNKS, 2):
+        for g in range(D_CHUNKS // PAIR):
             nc.sync.dma_start(
-                out=aw_sb[:, c : c + 2, :],
-                in_=aW[c * P : (c + 2) * P, :].rearrange("(r p) k -> p r k", p=P),
+                out=aw_sb[:, PAIR * g : PAIR * (g + 1), :].rearrange("m e k -> m (e k)"),
+                in_=pair_rows(aW)[:, g, :],
             )
         nc.sync.dma_start(out=stack[:, 0, :], in_=protos[0:P, :])
 
@@ -83,7 +96,7 @@ def tile_prototypelearnerv4_pa_s_kernel(
         x_grouped = keep.tile([P, X_PASSES, B, PACK], BF16, align_bytes=64)
 
         q_tab = keep.tile([P, D_CHUNKS, 2 * P], F32)
-        neg_half_q = keep.tile([P, D_CHUNKS, 2 * P], F32)
+        neg_half_q = keep.tile([P, SCALAR_CHUNKS, N_PROTO], F32)
         featT = keep.tile([P, D_CHUNKS, B], F32)
 
         with (
@@ -91,82 +104,118 @@ def tile_prototypelearnerv4_pa_s_kernel(
             tc.psum_pool(name="psum_mx", bufs=1) as psum_mx,
         ):
 
-            def transpose_four(src):
-                xt = psum_t.tile([P, PACK, P], BF16)
-                for t in range(PACK):
-                    nc.tensor.transpose(xt[:, t, :], src[:, t * P : (t + 1) * P], ident_bf[:])
+            def transpose_words(src):
+                words = src.bitcast(F32)
+                xt = psum_t.tile([P, 2, PAIR, P], F32, tag="xt")
+                for s in range(2):
+                    for u in range(PAIR):
+                        nc.tensor.transpose(
+                            xt[:, s, u, :], words[:, s, u * P : (u + 1) * P], ident_f32[:]
+                        )
                 return xt
 
             def quantise(grouped, codes, scales):
-                nc.vector.quantize_mx(
-                    out=codes.bitcast(FP8X4),
-                    scales=scales,
-                    in_=grouped.rearrange("p r t -> p (r t)"),
-                )
+                nc.vector.quantize_mx(out=codes.bitcast(FP8X4), scales=scales, in_=grouped)
 
-            def to_mx_operand(index, src, grouped, codes, scales):
-                xt = transpose_four(src)
-                permuted = xt[:].rearrange("p t r -> p r t")
-                if index % 3 == 2:
-                    nc.vector.tensor_copy(out=grouped, in_=permuted)
+            def to_mx_operands(index, src, grouped, codes, scales):
+                xt = transpose_words(src)
+                permuted = xt[:].rearrange("p s u r -> p s r u")
+                if index % 4 == 3:
+                    nc.vector.tensor_copy(out=grouped.bitcast(F32), in_=permuted)
                 else:
-                    nc.scalar.copy(out=grouped, in_=permuted)
-                quantise(grouped, codes, scales)
+                    nc.scalar.copy(out=grouped.bitcast(F32), in_=permuted)
+                quantise(
+                    grouped.rearrange("p s r t -> p (s r t)"),
+                    codes.rearrange("p s r -> p (s r)"),
+                    scales.rearrange("p s r -> p (s r)"),
+                )
 
             def new_grouped():
-                grouped = stage.tile([P, P, PACK], BF16, align_bytes=64)
+                grouped = stage.tile([P, 2, P, PACK], BF16, align_bytes=64)
                 return grouped[:]
 
-            z_sb = keep.tile([P, F1], BF16)
-            nc.vector.tensor_tensor(out=z_sb[:], in0=h_up_sb[:], in1=h_skip_sb[:], op=ALU.add)
-            to_mx_operand(0, z_sb[:], new_grouped(), z_codes[:], z_scales[:])
-            for r in range(F0_CHUNKS):
-                to_mx_operand(
-                    r, wu2_sb[:, r, :], new_grouped(), wu2_codes[:, r, :], wu2_scales[:, r, :]
+            z_sorted = keep.tile([P, PAIR, F1 // PAIR], BF16)
+            nc.vector.tensor_tensor(
+                out=z_sorted[:],
+                in0=h_up_sb[:].rearrange("b (w e) -> b e w", e=PAIR),
+                in1=h_skip_sb[:].rearrange("b (w e) -> b e w", e=PAIR),
+                op=ALU.add,
+            )
+            zt = psum_t.tile([P, PAIR, PAIR, B], BF16, tag="xt")
+            for u in range(PAIR):
+                for e in range(PAIR):
+                    nc.tensor.transpose(
+                        zt[:, u, e, :], z_sorted[:, e, u * P : (u + 1) * P], ident_bf[:]
+                    )
+            z_grouped = keep.tile([P, B, PACK], BF16, align_bytes=64)
+            nc.scalar.copy(
+                out=z_grouped[:],
+                in_=zt[:].rearrange("p u e b -> p (u e) b").rearrange("p t b -> p b t"),
+            )
+            quantise(z_grouped[:].rearrange("p b t -> p (b t)"), z_codes[:], z_scales[:])
+
+            for c in range(0, F0_CHUNKS, 2):
+                to_mx_operands(
+                    c // 2,
+                    wu2_sb[:, c : c + 2, :],
+                    new_grouped(),
+                    wu2_codes[:, c : c + 2, :],
+                    wu2_scales[:, c : c + 2, :],
                 )
 
-            for half in range(2):
-                xt = transpose_four(stack[:, 1, half * K_PASS : (half + 1) * K_PASS])
+            def stack_to_table(half):
+                xt = transpose_words(stack[:, half, :].rearrange("r (s k) -> r s k", s=2))
                 nc.scalar.copy(
-                    out=q_tab[:, half * PACK : (half + 1) * PACK, P : 2 * P], in_=xt[:]
+                    out=q_tab[:, :, half * P : (half + 1) * P].rearrange(
+                        "p (g e) r -> p g e r", e=PAIR
+                    ),
+                    in_=xt[:]
+                    .rearrange("p s u r -> p (s u) r")
+                    .bitcast(BF16)
+                    .rearrange("p g (r e) -> p g e r", e=PAIR),
                 )
+
+            stack_to_table(1)
 
             u2_ps = psum_mx.tile([P, F0_CHUNKS, B], F32)
-            for r in range(F0_CHUNKS):
+            for c in range(F0_CHUNKS):
                 nc.tensor.matmul_mx(
-                    out=u2_ps[:, r, :],
-                    lhsT=wu2_codes[:, r, :].bitcast(FP8X4),
-                    lhsT_scale=wu2_scales[:, r, :],
+                    out=u2_ps[:, c, :],
+                    lhsT=wu2_codes[:, c, :].bitcast(FP8X4),
+                    lhsT_scale=wu2_scales[:, c, :],
                     rhs=z_codes[:].bitcast(FP8X4),
                     rhs_scale=z_scales[:],
                     start=True,
                     stop=True,
                 )
             u2_bf = keep.tile([P, F0_CHUNKS, B], BF16)
-            for r in range(F0_CHUNKS):
+            for c in range(F0_CHUNKS):
                 nc.scalar.activation(
-                    out=u2_bf[:, r, :],
-                    in_=u2_ps[:, r, :],
+                    out=u2_bf[:, c, :],
+                    in_=u2_ps[:, c, :],
                     func=ACT.Relu,
-                    bias=q_tab[:, r, BU2_COL : BU2_COL + 1],
+                    bias=q_tab[:, c, BU2_COL : BU2_COL + 1],
                     scale=1.0,
                 )
-            u2_grouped = new_grouped()
-            nc.vector.tensor_copy(out=u2_grouped, in_=u2_bf[:].rearrange("p t r -> p r t"))
-            quantise(u2_grouped, u2_codes[:], u2_scales[:])
+            u2_grouped = keep.tile([P, B, PACK], BF16, align_bytes=64)
+            nc.vector.tensor_copy(out=u2_grouped[:], in_=u2_bf[:].rearrange("p t b -> p b t"))
+            quantise(u2_grouped[:].rearrange("p b t -> p (b t)"), u2_codes[:], u2_scales[:])
 
-            for c in range(D_CHUNKS):
-                to_mx_operand(
-                    c, wu3_sb[:, c, :], new_grouped(), wu3_codes[:, c, :], wu3_scales[:, c, :]
+            for c in range(0, D_CHUNKS, 2):
+                to_mx_operands(
+                    c // 2,
+                    wu3_sb[:, c : c + 2, :],
+                    new_grouped(),
+                    wu3_codes[:, c : c + 2, :],
+                    wu3_scales[:, c : c + 2, :],
                 )
-            for g in range(X_PASSES):
-                to_mx_operand(
-                    g,
-                    x_sb[:, g * K_PASS : (g + 1) * K_PASS],
-                    x_grouped[:, g, :, :],
-                    x_codes[:, g, :],
-                    x_scales[:, g, :],
-                )
+            to_mx_operands(
+                0,
+                x_sb[:].rearrange("b (s k) -> b s k", s=X_PASSES),
+                x_grouped[:],
+                x_codes[:],
+                x_scales[:],
+            )
             u3_ps = [
                 psum_mx.tile([P, BANK_CHUNKS, B], F32, name="u3_ps%d" % bank) for bank in range(2)
             ]
@@ -200,34 +249,35 @@ def tile_prototypelearnerv4_pa_s_kernel(
                 )
 
             for c in range(D_CHUNKS):
-                for g in range(X_PASSES):
-                    to_mx_operand(
-                        c * X_PASSES + g,
-                        aw_sb[:, c, g * K_PASS : (g + 1) * K_PASS],
-                        new_grouped(),
-                        aw_codes[:, c, g, :],
-                        aw_scales[:, c, g, :],
-                    )
-            for half in range(2):
-                xt = transpose_four(stack[:, 0, half * K_PASS : (half + 1) * K_PASS])
-                nc.scalar.copy(out=q_tab[:, half * PACK : (half + 1) * PACK, 0:P], in_=xt[:])
+                to_mx_operands(
+                    c,
+                    aw_sb[:, c, :].rearrange("m (s k) -> m s k", s=X_PASSES),
+                    new_grouped(),
+                    aw_codes[:, c, :, :],
+                    aw_scales[:, c, :, :],
+                )
+            stack_to_table(0)
             nc.vector.tensor_scalar(
-                out=neg_half_q[:], in0=q_tab[:], scalar1=-0.5, scalar2=None, op0=ALU.mult
+                out=neg_half_q[:],
+                in0=q_tab[:, 0:SCALAR_CHUNKS, 0:N_PROTO],
+                scalar1=-0.5,
+                scalar2=None,
+                op0=ALU.mult,
             )
 
             ad_ps = [
                 psum_mx.tile([P, BANK_CHUNKS, B], F32, name="ad_ps%d" % bank) for bank in range(2)
             ]
             for c in range(D_CHUNKS):
-                for g in range(X_PASSES):
+                for s in range(X_PASSES):
                     nc.tensor.matmul_mx(
                         out=ad_ps[c // BANK_CHUNKS][:, c % BANK_CHUNKS, :],
-                        lhsT=aw_codes[:, c, g, :].bitcast(FP8X4),
-                        lhsT_scale=aw_scales[:, c, g, :],
-                        rhs=x_codes[:, g, :].bitcast(FP8X4),
-                        rhs_scale=x_scales[:, g, :],
-                        start=(g == 0),
-                        stop=(g == X_PASSES - 1),
+                        lhsT=aw_codes[:, c, s, :].bitcast(FP8X4),
+                        lhsT_scale=aw_scales[:, c, s, :],
+                        rhs=x_codes[:, s, :].bitcast(FP8X4),
+                        rhs_scale=x_scales[:, s, :],
+                        start=(s == 0),
+                        stop=(s == X_PASSES - 1),
                     )
             for bank in range(2):
                 chunks = slice(bank * BANK_CHUNKS, (bank + 1) * BANK_CHUNKS)
@@ -235,7 +285,10 @@ def tile_prototypelearnerv4_pa_s_kernel(
                     out=featT[:, chunks, :], in0=ad_ps[bank][:], in1=rest[:, chunks, :], op=ALU.add
                 )
 
-        with tc.psum_pool(name="psum_acc", bufs=6) as psum_acc:
+        with (
+            tc.psum_pool(name="psum_once", bufs=1) as psum_once,
+            tc.psum_pool(name="psum_acc", bufs=6) as psum_acc,
+        ):
 
             def add_transposed(acc_slot, tile_in, first, last):
                 nc.tensor.matmul(
@@ -247,12 +300,29 @@ def tile_prototypelearnerv4_pa_s_kernel(
                     is_transpose=True,
                 )
 
+            vector_chunks = range(SCALAR_CHUNKS, D_CHUNKS)
+
+            proto_sums = psum_once.tile([P, 2 * P], F32)
+            for c in vector_chunks:
+                nc.tensor.matmul(
+                    out=proto_sums[:],
+                    lhsT=ones_f32[:],
+                    rhs=q_tab[:, c, :],
+                    start=(c == SCALAR_CHUNKS),
+                    stop=(c == D_CHUNKS - 1),
+                )
+            feat_cols = psum_once.tile([P, B], F32)
+            for c in vector_chunks:
+                add_transposed(feat_cols[:], featT[:, c, :], c == SCALAR_CHUNKS, c == D_CHUNKS - 1)
             feat_sum = keep.tile([P, 1], F32)
-            acc = psum_acc.tile([P, BANK_CHUNKS, B], F32)
-            for c in range(SCALAR_CHUNKS, D_CHUNKS):
-                add_transposed(acc[:, 0, :], featT[:, c, :], c == SCALAR_CHUNKS, c == D_CHUNKS - 1)
-            nc.vector.tensor_reduce(
-                out=feat_sum[:], in_=acc[:, 0, :], axis=mybir.AxisListType.X, op=ALU.add
+            nc.vector.tensor_reduce(out=feat_sum[:], in_=feat_cols[:], axis=AXIS_X, op=ALU.add)
+            correction = keep.tile([P, N_PROTO], F32)
+            nc.vector.tensor_scalar(
+                out=correction[:],
+                in0=proto_sums[:, 0:N_PROTO],
+                scalar1=feat_sum[:, 0:1],
+                scalar2=None,
+                op0=ALU.add,
             )
 
             half_sums = keep.tile([P, N_PROTO], F32)
@@ -260,42 +330,43 @@ def tile_prototypelearnerv4_pa_s_kernel(
                 acc = psum_acc.tile([P, BANK_CHUNKS, B], F32)
                 for slot in range(BANK_CHUNKS):
                     proto = first_proto + slot
-                    for c in range(D_CHUNKS):
-                        if c < SCALAR_CHUNKS:
-                            half_abs = work.tile([P, B], F32)
-                            nc.scalar.activation(
-                                out=half_abs[:],
-                                in_=featT[:, c, :],
-                                func=ACT.Abs,
-                                bias=neg_half_q[:, c, proto : proto + 1],
-                                scale=0.5,
-                            )
-                            term = half_abs
-                        else:
-                            half_max = work.tile([P, B], F32)
-                            nc.vector.tensor_scalar(
-                                out=half_max[:],
-                                in0=featT[:, c, :],
-                                scalar1=q_tab[:, c, proto : proto + 1],
-                                scalar2=neg_half_q[:, c, proto : proto + 1],
-                                op0=ALU.max,
-                                op1=ALU.add,
-                            )
-                            term = half_max
-                        add_transposed(acc[:, slot, :], term[:], c == 0, c == D_CHUNKS - 1)
+                    terms = []
+                    for c in range(SCALAR_CHUNKS):
+                        half_abs = abs_tiles.tile([P, B], F32)
+                        nc.scalar.activation(
+                            out=half_abs[:],
+                            in_=featT[:, c, :],
+                            func=ACT.Abs,
+                            bias=neg_half_q[:, c, proto : proto + 1],
+                            scale=0.5,
+                        )
+                        terms.append(half_abs)
+                    for c in vector_chunks:
+                        with_max = sum_tiles.tile([P, B], F32)
+                        nc.vector.scalar_tensor_tensor(
+                            out=with_max[:],
+                            in0=featT[:, c, :],
+                            scalar=q_tab[:, c, proto : proto + 1],
+                            in1=terms[c - SCALAR_CHUNKS][:],
+                            op0=ALU.max,
+                            op1=ALU.add,
+                        )
+                        terms[c - SCALAR_CHUNKS] = with_max
+                    for i in range(SCALAR_CHUNKS):
+                        add_transposed(acc[:, slot, :], terms[i][:], i == 0, i == SCALAR_CHUNKS - 1)
                 nc.vector.tensor_reduce(
                     out=half_sums[:, first_proto : first_proto + BANK_CHUNKS],
                     in_=acc[:],
-                    axis=mybir.AxisListType.X,
+                    axis=AXIS_X,
                     op=ALU.add,
                 )
 
             result = keep.tile([P, N_PROTO], F32)
-            nc.vector.tensor_scalar(
+            nc.vector.scalar_tensor_tensor(
                 out=result[:],
                 in0=half_sums[:],
-                scalar1=-2.0,
-                scalar2=feat_sum[:, 0:1],
+                scalar=-2.0,
+                in1=correction[:],
                 op0=ALU.mult,
                 op1=ALU.add,
             )

@@ -41,8 +41,7 @@ def tile_prototypelearnerv4_pa_s_kernel(
     with (
         tc.tile_pool(name="keep", bufs=1) as keep,
         tc.tile_pool(name="stage", bufs=4) as stage,
-        tc.tile_pool(name="abs_tiles", bufs=20) as abs_tiles,
-        tc.tile_pool(name="sum_tiles", bufs=12) as sum_tiles,
+        tc.tile_pool(name="terms_pool", bufs=20) as terms_pool,
     ):
         ident_bf = keep.tile([P, P], BF16)
         make_identity(nc, ident_bf[:])
@@ -332,26 +331,25 @@ def tile_prototypelearnerv4_pa_s_kernel(
                     proto = first_proto + slot
                     terms = []
                     for c in range(SCALAR_CHUNKS):
-                        half_abs = abs_tiles.tile([P, B], F32)
+                        term = terms_pool.tile([P, B], F32)
                         nc.scalar.activation(
-                            out=half_abs[:],
+                            out=term[:],
                             in_=featT[:, c, :],
                             func=ACT.Abs,
                             bias=neg_half_q[:, c, proto : proto + 1],
                             scale=0.5,
                         )
-                        terms.append(half_abs)
+                        terms.append(term)
                     for c in vector_chunks:
-                        with_max = sum_tiles.tile([P, B], F32)
+                        term = terms[c - SCALAR_CHUNKS]
                         nc.vector.scalar_tensor_tensor(
-                            out=with_max[:],
+                            out=term[:],
                             in0=featT[:, c, :],
                             scalar=q_tab[:, c, proto : proto + 1],
-                            in1=terms[c - SCALAR_CHUNKS][:],
+                            in1=term[:],
                             op0=ALU.max,
                             op1=ALU.add,
                         )
-                        terms[c - SCALAR_CHUNKS] = with_max
                     for i in range(SCALAR_CHUNKS):
                         add_transposed(acc[:, slot, :], terms[i][:], i == 0, i == SCALAR_CHUNKS - 1)
                 nc.vector.tensor_reduce(

@@ -24,7 +24,8 @@ BANK_CHUNKS = 4
 AB_ROW, BU3_ROW, BU2_ROW = 72, 73, 74
 AB_COL, BU3_COL, BU2_COL = P + AB_ROW, P + BU3_ROW, P + BU2_ROW
 
-SCALAR_CHUNKS = 5
+SCALAR_CHUNKS = 4
+ADDED_CHUNKS = 3
 
 FLOPS = 2 * B * (F1 * F0 + F0 * D + D * D) + 3 * B * N_PROTO * D
 
@@ -41,7 +42,8 @@ def tile_prototypelearnerv4_pa_s_kernel(
     with (
         tc.tile_pool(name="keep", bufs=1) as keep,
         tc.tile_pool(name="stage", bufs=4) as stage,
-        tc.tile_pool(name="terms_pool", bufs=20) as terms_pool,
+        tc.tile_pool(name="scalar_terms", bufs=20) as scalar_terms,
+        tc.tile_pool(name="vector_terms", bufs=6) as vector_terms,
     ):
         ident_bf = keep.tile([P, P], BF16)
         make_identity(nc, ident_bf[:])
@@ -68,6 +70,7 @@ def tile_prototypelearnerv4_pa_s_kernel(
         nc.sync.dma_start(
             out=wu2_sb[:].rearrange("m (g e) k -> m g (e k)", e=PAIR), in_=pair_rows(Wu2)
         )
+        nc.sync.dma_start(out=stack[:, 0, :], in_=protos[0:P, :])
         nc.sync.dma_start(
             out=wu3_sb[:].rearrange("m (g e) k -> m g (e k)", e=PAIR), in_=pair_rows(Wu3)
         )
@@ -77,7 +80,6 @@ def tile_prototypelearnerv4_pa_s_kernel(
                 out=aw_sb[:, PAIR * g : PAIR * (g + 1), :].rearrange("m e k -> m (e k)"),
                 in_=pair_rows(aW)[:, g, :],
             )
-        nc.sync.dma_start(out=stack[:, 0, :], in_=protos[0:P, :])
 
         z_codes = keep.tile([P, B], U32, align_bytes=64)
         z_scales = keep.tile([P, B], U8, align_bytes=64)
@@ -96,6 +98,7 @@ def tile_prototypelearnerv4_pa_s_kernel(
 
         q_tab = keep.tile([P, D_CHUNKS, 2 * P], F32)
         neg_half_q = keep.tile([P, SCALAR_CHUNKS, N_PROTO], F32)
+        proto_sums = keep.tile([P, N_PROTO], F32)
         featT = keep.tile([P, D_CHUNKS, B], F32)
 
         with (
@@ -200,6 +203,22 @@ def tile_prototypelearnerv4_pa_s_kernel(
             nc.vector.tensor_copy(out=u2_grouped[:], in_=u2_bf[:].rearrange("p t b -> p b t"))
             quantise(u2_grouped[:].rearrange("p b t -> p (b t)"), u2_codes[:], u2_scales[:])
 
+            stack_to_table(0)
+            nc.vector.tensor_scalar(
+                out=neg_half_q[:],
+                in0=q_tab[:, 0:SCALAR_CHUNKS, 0:N_PROTO],
+                scalar1=-0.5,
+                scalar2=None,
+                op0=ALU.mult,
+            )
+            q_upper = keep.tile([P, 2 * P], F32)
+            nc.vector.tensor_reduce(
+                out=q_upper[:],
+                in_=q_tab[:, SCALAR_CHUNKS:D_CHUNKS, :].rearrange("p c r -> p r c"),
+                axis=AXIS_X,
+                op=ALU.add,
+            )
+
             for c in range(0, D_CHUNKS, 2):
                 to_mx_operands(
                     c // 2,
@@ -247,42 +266,45 @@ def tile_prototypelearnerv4_pa_s_kernel(
                     op1=ALU.add,
                 )
 
-            for c in range(D_CHUNKS):
-                to_mx_operands(
-                    c,
-                    aw_sb[:, c, :].rearrange("m (s k) -> m s k", s=X_PASSES),
-                    new_grouped(),
-                    aw_codes[:, c, :, :],
-                    aw_scales[:, c, :, :],
-                )
-            stack_to_table(0)
-            nc.vector.tensor_scalar(
-                out=neg_half_q[:],
-                in0=q_tab[:, 0:SCALAR_CHUNKS, 0:N_PROTO],
-                scalar1=-0.5,
-                scalar2=None,
-                op0=ALU.mult,
-            )
-
-            ad_ps = [
-                psum_mx.tile([P, BANK_CHUNKS, B], F32, name="ad_ps%d" % bank) for bank in range(2)
-            ]
-            for c in range(D_CHUNKS):
-                for s in range(X_PASSES):
-                    nc.tensor.matmul_mx(
-                        out=ad_ps[c // BANK_CHUNKS][:, c % BANK_CHUNKS, :],
-                        lhsT=aw_codes[:, c, s, :].bitcast(FP8X4),
-                        lhsT_scale=aw_scales[:, c, s, :],
-                        rhs=x_codes[:, s, :].bitcast(FP8X4),
-                        rhs_scale=x_scales[:, s, :],
-                        start=(s == 0),
-                        stop=(s == X_PASSES - 1),
+            def adapter_operands(first):
+                for c in range(first, first + BANK_CHUNKS):
+                    to_mx_operands(
+                        c,
+                        aw_sb[:, c, :].rearrange("m (s k) -> m s k", s=X_PASSES),
+                        new_grouped(),
+                        aw_codes[:, c, :, :],
+                        aw_scales[:, c, :, :],
                     )
-            for bank in range(2):
-                chunks = slice(bank * BANK_CHUNKS, (bank + 1) * BANK_CHUNKS)
+
+            def features(first):
+                ad_ps = psum_mx.tile([P, BANK_CHUNKS, B], F32, name="ad_ps%d" % first)
+                for c in range(first, first + BANK_CHUNKS):
+                    for s in range(X_PASSES):
+                        nc.tensor.matmul_mx(
+                            out=ad_ps[:, c - first, :],
+                            lhsT=aw_codes[:, c, s, :].bitcast(FP8X4),
+                            lhsT_scale=aw_scales[:, c, s, :],
+                            rhs=x_codes[:, s, :].bitcast(FP8X4),
+                            rhs_scale=x_scales[:, s, :],
+                            start=(s == 0),
+                            stop=(s == X_PASSES - 1),
+                        )
                 nc.vector.tensor_tensor(
-                    out=featT[:, chunks, :], in0=ad_ps[bank][:], in1=rest[:, chunks, :], op=ALU.add
+                    out=featT[:, first : first + BANK_CHUNKS, :],
+                    in0=ad_ps[:],
+                    in1=rest[:, first : first + BANK_CHUNKS, :],
+                    op=ALU.add,
                 )
+
+            adapter_operands(0)
+            features(0)
+            adapter_operands(BANK_CHUNKS)
+            proto_sums_ps = psum_mx.tile([P, 2 * P], F32, tag="u2_ps")
+            nc.tensor.matmul(
+                out=proto_sums_ps[:], lhsT=ones_f32[:], rhs=q_upper[:], start=True, stop=True
+            )
+            nc.scalar.copy(out=proto_sums[:], in_=proto_sums_ps[:, 0:N_PROTO])
+            features(BANK_CHUNKS)
 
         with (
             tc.psum_pool(name="psum_once", bufs=1) as psum_once,
@@ -299,26 +321,15 @@ def tile_prototypelearnerv4_pa_s_kernel(
                     is_transpose=True,
                 )
 
-            vector_chunks = range(SCALAR_CHUNKS, D_CHUNKS)
-
-            proto_sums = psum_once.tile([P, 2 * P], F32)
-            for c in vector_chunks:
-                nc.tensor.matmul(
-                    out=proto_sums[:],
-                    lhsT=ones_f32[:],
-                    rhs=q_tab[:, c, :],
-                    start=(c == SCALAR_CHUNKS),
-                    stop=(c == D_CHUNKS - 1),
-                )
             feat_cols = psum_once.tile([P, B], F32)
-            for c in vector_chunks:
+            for c in range(SCALAR_CHUNKS, D_CHUNKS):
                 add_transposed(feat_cols[:], featT[:, c, :], c == SCALAR_CHUNKS, c == D_CHUNKS - 1)
             feat_sum = keep.tile([P, 1], F32)
             nc.vector.tensor_reduce(out=feat_sum[:], in_=feat_cols[:], axis=AXIS_X, op=ALU.add)
             correction = keep.tile([P, N_PROTO], F32)
             nc.vector.tensor_scalar(
                 out=correction[:],
-                in0=proto_sums[:, 0:N_PROTO],
+                in0=proto_sums[:],
                 scalar1=feat_sum[:, 0:1],
                 scalar2=None,
                 op0=ALU.add,
@@ -331,7 +342,7 @@ def tile_prototypelearnerv4_pa_s_kernel(
                     proto = first_proto + slot
                     terms = []
                     for c in range(SCALAR_CHUNKS):
-                        term = terms_pool.tile([P, B], F32)
+                        term = scalar_terms.tile([P, B], F32)
                         nc.scalar.activation(
                             out=term[:],
                             in_=featT[:, c, :],
@@ -340,18 +351,29 @@ def tile_prototypelearnerv4_pa_s_kernel(
                             scale=0.5,
                         )
                         terms.append(term)
-                    for c in vector_chunks:
-                        term = terms[c - SCALAR_CHUNKS]
-                        nc.vector.scalar_tensor_tensor(
-                            out=term[:],
-                            in0=featT[:, c, :],
-                            scalar=q_tab[:, c, proto : proto + 1],
-                            in1=term[:],
-                            op0=ALU.max,
-                            op1=ALU.add,
-                        )
-                    for i in range(SCALAR_CHUNKS):
-                        add_transposed(acc[:, slot, :], terms[i][:], i == 0, i == SCALAR_CHUNKS - 1)
+                    for i in range(D_CHUNKS - SCALAR_CHUNKS):
+                        c = SCALAR_CHUNKS + i
+                        if i < ADDED_CHUNKS:
+                            nc.vector.scalar_tensor_tensor(
+                                out=terms[i][:],
+                                in0=featT[:, c, :],
+                                scalar=q_tab[:, c, proto : proto + 1],
+                                in1=terms[i][:],
+                                op0=ALU.max,
+                                op1=ALU.add,
+                            )
+                        else:
+                            own_term = vector_terms.tile([P, B], F32)
+                            nc.vector.tensor_scalar(
+                                out=own_term[:],
+                                in0=featT[:, c, :],
+                                scalar1=q_tab[:, c, proto : proto + 1],
+                                scalar2=None,
+                                op0=ALU.max,
+                            )
+                            terms.append(own_term)
+                    for i in range(len(terms)):
+                        add_transposed(acc[:, slot, :], terms[i][:], i == 0, i == len(terms) - 1)
                 nc.vector.tensor_reduce(
                     out=half_sums[:, first_proto : first_proto + BANK_CHUNKS],
                     in_=acc[:],

@@ -24,8 +24,10 @@ BANK_CHUNKS = 4
 AB_ROW, BU3_ROW, BU2_ROW = 72, 73, 74
 AB_COL, BU3_COL, BU2_COL = P + AB_ROW, P + BU3_ROW, P + BU2_ROW
 
-SCALAR_CHUNKS = 4
-ADDED_CHUNKS = 3
+DIRECT = 80
+DIRECT_LOAD = 4
+GROUPS = (N_PROTO - DIRECT) // BANK_CHUNKS
+SCALAR_CHUNKS = 6
 
 FLOPS = 2 * B * (F1 * F0 + F0 * D + D * D) + 3 * B * N_PROTO * D
 
@@ -42,8 +44,10 @@ def tile_prototypelearnerv4_pa_s_kernel(
     with (
         tc.tile_pool(name="keep", bufs=1) as keep,
         tc.tile_pool(name="stage", bufs=4) as stage,
-        tc.tile_pool(name="scalar_terms", bufs=20) as scalar_terms,
-        tc.tile_pool(name="vector_terms", bufs=6) as vector_terms,
+        tc.tile_pool(name="scalar_terms", bufs=30) as scalar_terms,
+        tc.tile_pool(name="vector_terms", bufs=20) as vector_terms,
+        tc.tile_pool(name="direct_q", bufs=4) as direct_q,
+        tc.tile_pool(name="direct_terms", bufs=2) as direct_terms,
     ):
         ident_bf = keep.tile([P, P], BF16)
         make_identity(nc, ident_bf[:])
@@ -97,7 +101,7 @@ def tile_prototypelearnerv4_pa_s_kernel(
         x_grouped = keep.tile([P, X_PASSES, B, PACK], BF16, align_bytes=64)
 
         q_tab = keep.tile([P, D_CHUNKS, 2 * P], F32)
-        neg_half_q = keep.tile([P, SCALAR_CHUNKS, N_PROTO], F32)
+        neg_half_q = keep.tile([P, SCALAR_CHUNKS, N_PROTO - DIRECT], F32)
         proto_sums = keep.tile([P, N_PROTO], F32)
         featT = keep.tile([P, D_CHUNKS, B], F32)
 
@@ -206,15 +210,21 @@ def tile_prototypelearnerv4_pa_s_kernel(
             stack_to_table(0)
             nc.vector.tensor_scalar(
                 out=neg_half_q[:],
-                in0=q_tab[:, 0:SCALAR_CHUNKS, 0:N_PROTO],
+                in0=q_tab[:, 0:SCALAR_CHUNKS, DIRECT:N_PROTO],
                 scalar1=-0.5,
                 scalar2=None,
                 op0=ALU.mult,
             )
             q_upper = keep.tile([P, 2 * P], F32)
             nc.vector.tensor_reduce(
-                out=q_upper[:],
-                in_=q_tab[:, SCALAR_CHUNKS:D_CHUNKS, :].rearrange("p c r -> p r c"),
+                out=q_upper[:, 0:DIRECT],
+                in_=q_tab[:, :, 0:DIRECT].rearrange("p c r -> p r c"),
+                axis=AXIS_X,
+                op=ALU.add,
+            )
+            nc.vector.tensor_reduce(
+                out=q_upper[:, DIRECT : 2 * P],
+                in_=q_tab[:, SCALAR_CHUNKS:D_CHUNKS, DIRECT : 2 * P].rearrange("p c r -> p r c"),
                 axis=AXIS_X,
                 op=ALU.add,
             )
@@ -321,25 +331,67 @@ def tile_prototypelearnerv4_pa_s_kernel(
                     is_transpose=True,
                 )
 
-            feat_cols = psum_once.tile([P, B], F32)
-            for c in range(SCALAR_CHUNKS, D_CHUNKS):
-                add_transposed(feat_cols[:], featT[:, c, :], c == SCALAR_CHUNKS, c == D_CHUNKS - 1)
-            feat_sum = keep.tile([P, 1], F32)
-            nc.vector.tensor_reduce(out=feat_sum[:], in_=feat_cols[:], axis=AXIS_X, op=ALU.add)
+            feat_rows = keep.tile([P, D], F32)
+            row_sums = keep.tile([P, 4], F32)
+            for half in range(2):
+                feat_ps = psum_once.tile([P, BANK_CHUNKS, P], F32, name="feat_ps%d" % half)
+                for i in range(BANK_CHUNKS):
+                    add_transposed(feat_ps[:, i, :], featT[:, half * BANK_CHUNKS + i, :], True, True)
+                nc.scalar.activation(
+                    out=feat_rows[:, half * (D // 2) : (half + 1) * (D // 2)].rearrange(
+                        "b (g p e) -> b g p e", g=BANK_CHUNKS // PAIR, e=PAIR
+                    ),
+                    in_=feat_ps[:].rearrange("b (g e) p -> b g p e", e=PAIR),
+                    func=ACT.Copy,
+                    accum_out=row_sums[:, half : half + 1],
+                )
+            nc.vector.tensor_reduce(
+                out=row_sums[:, 2:3],
+                in_=feat_ps[:, SCALAR_CHUNKS - BANK_CHUNKS : BANK_CHUNKS, :].rearrange(
+                    "b c p -> b (c p)"
+                ),
+                axis=AXIS_X,
+                op=ALU.add,
+            )
+            nc.vector.tensor_tensor(
+                out=row_sums[:, 3:4], in0=row_sums[:, 0:1], in1=row_sums[:, 1:2], op=ALU.add
+            )
             correction = keep.tile([P, N_PROTO], F32)
             nc.vector.tensor_scalar(
-                out=correction[:],
-                in0=proto_sums[:],
-                scalar1=feat_sum[:, 0:1],
+                out=correction[:, 0:DIRECT],
+                in0=proto_sums[:, 0:DIRECT],
+                scalar1=row_sums[:, 3:4],
+                scalar2=None,
+                op0=ALU.add,
+            )
+            nc.vector.tensor_scalar(
+                out=correction[:, DIRECT:N_PROTO],
+                in0=proto_sums[:, DIRECT:N_PROTO],
+                scalar1=row_sums[:, 2:3],
                 scalar2=None,
                 op0=ALU.add,
             )
 
             half_sums = keep.tile([P, N_PROTO], F32)
-            for first_proto in range(0, N_PROTO, BANK_CHUNKS):
+
+            def direct(proto):
+                junk = direct_terms.tile([P, D], F32)
+                nc.vector.scalar_tensor_tensor(
+                    out=junk[:],
+                    in0=q_rows[proto // DIRECT_LOAD][:, proto % DIRECT_LOAD, :],
+                    scalar=1.0,
+                    in1=feat_rows[:],
+                    op0=ALU.mult,
+                    op1=ALU.max,
+                    accum_out=half_sums[:, proto : proto + 1],
+                )
+
+            q_rows = []
+            for group in range(GROUPS):
                 acc = psum_acc.tile([P, BANK_CHUNKS, B], F32)
                 for slot in range(BANK_CHUNKS):
-                    proto = first_proto + slot
+                    index = group * BANK_CHUNKS + slot
+                    proto = DIRECT + index
                     terms = []
                     for c in range(SCALAR_CHUNKS):
                         term = scalar_terms.tile([P, B], F32)
@@ -347,33 +399,34 @@ def tile_prototypelearnerv4_pa_s_kernel(
                             out=term[:],
                             in_=featT[:, c, :],
                             func=ACT.Abs,
-                            bias=neg_half_q[:, c, proto : proto + 1],
+                            bias=neg_half_q[:, c, index : index + 1],
                             scale=0.5,
                         )
                         terms.append(term)
-                    for i in range(D_CHUNKS - SCALAR_CHUNKS):
-                        c = SCALAR_CHUNKS + i
-                        if i < ADDED_CHUNKS:
-                            nc.vector.scalar_tensor_tensor(
-                                out=terms[i][:],
-                                in0=featT[:, c, :],
-                                scalar=q_tab[:, c, proto : proto + 1],
-                                in1=terms[i][:],
-                                op0=ALU.max,
-                                op1=ALU.add,
-                            )
-                        else:
-                            own_term = vector_terms.tile([P, B], F32)
-                            nc.vector.tensor_scalar(
-                                out=own_term[:],
-                                in0=featT[:, c, :],
-                                scalar1=q_tab[:, c, proto : proto + 1],
-                                scalar2=None,
-                                op0=ALU.max,
-                            )
-                            terms.append(own_term)
+                    for c in range(SCALAR_CHUNKS, D_CHUNKS):
+                        own_term = vector_terms.tile([P, B], F32)
+                        nc.vector.tensor_scalar(
+                            out=own_term[:],
+                            in0=featT[:, c, :],
+                            scalar1=q_tab[:, c, proto : proto + 1],
+                            scalar2=None,
+                            op0=ALU.max,
+                        )
+                        terms.append(own_term)
                     for i in range(len(terms)):
                         add_transposed(acc[:, slot, :], terms[i][:], i == 0, i == len(terms) - 1)
+                for proto in range(group * DIRECT // GROUPS, (group + 1) * DIRECT // GROUPS):
+                    if proto % DIRECT_LOAD == 0:
+                        q_load = direct_q.tile([P, DIRECT_LOAD, D], BF16)
+                        nc.sync.dma_start(
+                            out=q_load[:].rearrange("b r d -> b (r d)"),
+                            in_=protos[proto : proto + DIRECT_LOAD, :]
+                            .rearrange("r d -> (r d)")
+                            .partition_broadcast(P),
+                        )
+                        q_rows.append(q_load)
+                    direct(proto)
+                first_proto = DIRECT + group * BANK_CHUNKS
                 nc.vector.tensor_reduce(
                     out=half_sums[:, first_proto : first_proto + BANK_CHUNKS],
                     in_=acc[:],

@@ -21,13 +21,12 @@ F0_CHUNKS = F0 // P
 X_PASSES = D // K_PASS
 BANK_CHUNKS = 4
 
-AB_ROW, BU3_ROW, BU2_ROW = 72, 73, 74
-AB_COL, BU3_COL, BU2_COL = P + AB_ROW, P + BU3_ROW, P + BU2_ROW
 
-DIRECT = 80
+DIRECT = 100
 DIRECT_LOAD = 4
-GROUPS = (N_PROTO - DIRECT) // BANK_CHUNKS
-SCALAR_CHUNKS = 6
+TURNED = N_PROTO - DIRECT
+GROUPS = TURNED // BANK_CHUNKS
+AB_ROW, BU3_ROW, BU2_ROW = TURNED, TURNED + 1, TURNED + 2
 
 FLOPS = 2 * B * (F1 * F0 + F0 * D + D * D) + 3 * B * N_PROTO * D
 
@@ -45,7 +44,6 @@ def tile_prototypelearnerv4_pa_s_kernel(
         tc.tile_pool(name="keep", bufs=1) as keep,
         tc.tile_pool(name="stage", bufs=4) as stage,
         tc.tile_pool(name="scalar_terms", bufs=30) as scalar_terms,
-        tc.tile_pool(name="vector_terms", bufs=20) as vector_terms,
         tc.tile_pool(name="direct_q", bufs=4) as direct_q,
         tc.tile_pool(name="direct_terms", bufs=2) as direct_terms,
     ):
@@ -53,28 +51,27 @@ def tile_prototypelearnerv4_pa_s_kernel(
         make_identity(nc, ident_bf[:])
         ident_f32 = keep.tile([P, P], F32)
         make_identity(nc, ident_f32[:])
-        ones_f32 = keep.tile([P, P], F32)
-        nc.vector.memset(ones_f32[:], 1.0)
 
         h_up_sb = keep.tile([P, F1], BF16)
         h_skip_sb = keep.tile([P, F1], BF16)
-        stack = keep.tile([P, 2, D], BF16)
+        stack = keep.tile([P, D], BF16)
+        direct_rows = keep.tile([P, D], BF16)
         wu2_sb = keep.tile([P, F0_CHUNKS, F1], BF16)
         wu3_sb = keep.tile([P, D_CHUNKS, F0], BF16)
         x_sb = keep.tile([P, D], BF16)
         aw_sb = keep.tile([P, D_CHUNKS, D], BF16)
 
-        nc.vector.memset(stack[:, 1, :], 0.0)
+        nc.vector.memset(stack[:], 0.0)
+        nc.vector.memset(direct_rows[:], 0.0)
         nc.sync.dma_start(out=h_up_sb[:], in_=h_up)
         nc.sync.dma_start(out=h_skip_sb[:], in_=h_skip)
-        nc.sync.dma_start(out=stack[BU2_ROW : BU2_ROW + 1, 1, 0:F0], in_=bu2.unsqueeze(0))
-        nc.sync.dma_start(out=stack[BU3_ROW : BU3_ROW + 1, 1, :], in_=bu3.unsqueeze(0))
-        nc.sync.dma_start(out=stack[AB_ROW : AB_ROW + 1, 1, :], in_=ab.unsqueeze(0))
-        nc.sync.dma_start(out=stack[0 : N_PROTO - P, 1, :], in_=protos[P:N_PROTO, :])
+        nc.sync.dma_start(out=stack[BU2_ROW : BU2_ROW + 1, 0:F0], in_=bu2.unsqueeze(0))
+        nc.sync.dma_start(out=stack[BU3_ROW : BU3_ROW + 1, :], in_=bu3.unsqueeze(0))
+        nc.sync.dma_start(out=stack[AB_ROW : AB_ROW + 1, :], in_=ab.unsqueeze(0))
+        nc.sync.dma_start(out=stack[0:TURNED, :], in_=protos[DIRECT:N_PROTO, :])
         nc.sync.dma_start(
             out=wu2_sb[:].rearrange("m (g e) k -> m g (e k)", e=PAIR), in_=pair_rows(Wu2)
         )
-        nc.sync.dma_start(out=stack[:, 0, :], in_=protos[0:P, :])
         nc.sync.dma_start(
             out=wu3_sb[:].rearrange("m (g e) k -> m g (e k)", e=PAIR), in_=pair_rows(Wu3)
         )
@@ -84,6 +81,7 @@ def tile_prototypelearnerv4_pa_s_kernel(
                 out=aw_sb[:, PAIR * g : PAIR * (g + 1), :].rearrange("m e k -> m (e k)"),
                 in_=pair_rows(aW)[:, g, :],
             )
+        nc.sync.dma_start(out=direct_rows[0:DIRECT, :], in_=protos[0:DIRECT, :])
 
         z_codes = keep.tile([P, B], U32, align_bytes=64)
         z_scales = keep.tile([P, B], U8, align_bytes=64)
@@ -100,9 +98,8 @@ def tile_prototypelearnerv4_pa_s_kernel(
 
         x_grouped = keep.tile([P, X_PASSES, B, PACK], BF16, align_bytes=64)
 
-        q_tab = keep.tile([P, D_CHUNKS, 2 * P], F32)
-        neg_half_q = keep.tile([P, SCALAR_CHUNKS, N_PROTO - DIRECT], F32)
-        proto_sums = keep.tile([P, N_PROTO], F32)
+        q_tab = keep.tile([P, D_CHUNKS, P], F32)
+        neg_q = keep.tile([P, D_CHUNKS, TURNED], F32)
         featT = keep.tile([P, D_CHUNKS, B], F32)
 
         with (
@@ -169,19 +166,14 @@ def tile_prototypelearnerv4_pa_s_kernel(
                     wu2_scales[:, c : c + 2, :],
                 )
 
-            def stack_to_table(half):
-                xt = transpose_words(stack[:, half, :].rearrange("r (s k) -> r s k", s=2))
-                nc.scalar.copy(
-                    out=q_tab[:, :, half * P : (half + 1) * P].rearrange(
-                        "p (g e) r -> p g e r", e=PAIR
-                    ),
-                    in_=xt[:]
-                    .rearrange("p s u r -> p (s u) r")
-                    .bitcast(BF16)
-                    .rearrange("p g (r e) -> p g e r", e=PAIR),
-                )
-
-            stack_to_table(1)
+            stack_t = transpose_words(stack[:].rearrange("r (s k) -> r s k", s=2))
+            nc.scalar.copy(
+                out=q_tab[:].rearrange("p (g e) r -> p g e r", e=PAIR),
+                in_=stack_t[:]
+                .rearrange("p s u r -> p (s u) r")
+                .bitcast(BF16)
+                .rearrange("p g (r e) -> p g e r", e=PAIR),
+            )
 
             u2_ps = psum_mx.tile([P, F0_CHUNKS, B], F32)
             for c in range(F0_CHUNKS):
@@ -200,33 +192,19 @@ def tile_prototypelearnerv4_pa_s_kernel(
                     out=u2_bf[:, c, :],
                     in_=u2_ps[:, c, :],
                     func=ACT.Relu,
-                    bias=q_tab[:, c, BU2_COL : BU2_COL + 1],
+                    bias=q_tab[:, c, BU2_ROW : BU2_ROW + 1],
                     scale=1.0,
                 )
             u2_grouped = keep.tile([P, B, PACK], BF16, align_bytes=64)
             nc.vector.tensor_copy(out=u2_grouped[:], in_=u2_bf[:].rearrange("p t b -> p b t"))
             quantise(u2_grouped[:].rearrange("p b t -> p (b t)"), u2_codes[:], u2_scales[:])
 
-            stack_to_table(0)
             nc.vector.tensor_scalar(
-                out=neg_half_q[:],
-                in0=q_tab[:, 0:SCALAR_CHUNKS, DIRECT:N_PROTO],
-                scalar1=-0.5,
+                out=neg_q[:],
+                in0=q_tab[:, :, 0:TURNED],
+                scalar1=-1.0,
                 scalar2=None,
                 op0=ALU.mult,
-            )
-            q_upper = keep.tile([P, 2 * P], F32)
-            nc.vector.tensor_reduce(
-                out=q_upper[:, 0:DIRECT],
-                in_=q_tab[:, :, 0:DIRECT].rearrange("p c r -> p r c"),
-                axis=AXIS_X,
-                op=ALU.add,
-            )
-            nc.vector.tensor_reduce(
-                out=q_upper[:, DIRECT : 2 * P],
-                in_=q_tab[:, SCALAR_CHUNKS:D_CHUNKS, DIRECT : 2 * P].rearrange("p c r -> p r c"),
-                axis=AXIS_X,
-                op=ALU.add,
             )
 
             for c in range(0, D_CHUNKS, 2):
@@ -264,13 +242,13 @@ def tile_prototypelearnerv4_pa_s_kernel(
                     out=u3_sb[:, c, :],
                     in_=u3_ps[c // BANK_CHUNKS][:, c % BANK_CHUNKS, :],
                     func=ACT.Relu,
-                    bias=q_tab[:, c, BU3_COL : BU3_COL + 1],
+                    bias=q_tab[:, c, BU3_ROW : BU3_ROW + 1],
                     scale=1.0,
                 )
                 nc.vector.scalar_tensor_tensor(
                     out=rest[:, c, :],
                     in0=x_grouped[:, c // PACK, :, c % PACK],
-                    scalar=q_tab[:, c, AB_COL : AB_COL + 1],
+                    scalar=q_tab[:, c, AB_ROW : AB_ROW + 1],
                     in1=u3_sb[:, c, :],
                     op0=ALU.add,
                     op1=ALU.add,
@@ -309,11 +287,6 @@ def tile_prototypelearnerv4_pa_s_kernel(
             adapter_operands(0)
             features(0)
             adapter_operands(BANK_CHUNKS)
-            proto_sums_ps = psum_mx.tile([P, 2 * P], F32, tag="u2_ps")
-            nc.tensor.matmul(
-                out=proto_sums_ps[:], lhsT=ones_f32[:], rhs=q_upper[:], start=True, stop=True
-            )
-            nc.scalar.copy(out=proto_sums[:], in_=proto_sums_ps[:, 0:N_PROTO])
             features(BANK_CHUNKS)
 
         with (
@@ -332,7 +305,7 @@ def tile_prototypelearnerv4_pa_s_kernel(
                 )
 
             feat_rows = keep.tile([P, D], F32)
-            row_sums = keep.tile([P, 4], F32)
+            row_sums = keep.tile([P, 3], F32)
             for half in range(2):
                 feat_ps = psum_once.tile([P, BANK_CHUNKS, P], F32, name="feat_ps%d" % half)
                 for i in range(BANK_CHUNKS):
@@ -345,34 +318,8 @@ def tile_prototypelearnerv4_pa_s_kernel(
                     func=ACT.Copy,
                     accum_out=row_sums[:, half : half + 1],
                 )
-            nc.vector.tensor_reduce(
-                out=row_sums[:, 2:3],
-                in_=feat_ps[:, SCALAR_CHUNKS - BANK_CHUNKS : BANK_CHUNKS, :].rearrange(
-                    "b c p -> b (c p)"
-                ),
-                axis=AXIS_X,
-                op=ALU.add,
-            )
-            nc.vector.tensor_tensor(
-                out=row_sums[:, 3:4], in0=row_sums[:, 0:1], in1=row_sums[:, 1:2], op=ALU.add
-            )
-            correction = keep.tile([P, N_PROTO], F32)
-            nc.vector.tensor_scalar(
-                out=correction[:, 0:DIRECT],
-                in0=proto_sums[:, 0:DIRECT],
-                scalar1=row_sums[:, 3:4],
-                scalar2=None,
-                op0=ALU.add,
-            )
-            nc.vector.tensor_scalar(
-                out=correction[:, DIRECT:N_PROTO],
-                in0=proto_sums[:, DIRECT:N_PROTO],
-                scalar1=row_sums[:, 2:3],
-                scalar2=None,
-                op0=ALU.add,
-            )
 
-            half_sums = keep.tile([P, N_PROTO], F32)
+            sums = keep.tile([P, N_PROTO], F32)
 
             def direct(proto):
                 junk = direct_terms.tile([P, D], F32)
@@ -383,7 +330,7 @@ def tile_prototypelearnerv4_pa_s_kernel(
                     in1=feat_rows[:],
                     op0=ALU.mult,
                     op1=ALU.max,
-                    accum_out=half_sums[:, proto : proto + 1],
+                    accum_out=sums[:, proto : proto + 1],
                 )
 
             q_rows = []
@@ -391,30 +338,16 @@ def tile_prototypelearnerv4_pa_s_kernel(
                 acc = psum_acc.tile([P, BANK_CHUNKS, B], F32)
                 for slot in range(BANK_CHUNKS):
                     index = group * BANK_CHUNKS + slot
-                    proto = DIRECT + index
-                    terms = []
-                    for c in range(SCALAR_CHUNKS):
+                    for c in range(D_CHUNKS):
                         term = scalar_terms.tile([P, B], F32)
                         nc.scalar.activation(
                             out=term[:],
                             in_=featT[:, c, :],
                             func=ACT.Abs,
-                            bias=neg_half_q[:, c, index : index + 1],
-                            scale=0.5,
+                            bias=neg_q[:, c, index : index + 1],
+                            scale=1.0,
                         )
-                        terms.append(term)
-                    for c in range(SCALAR_CHUNKS, D_CHUNKS):
-                        own_term = vector_terms.tile([P, B], F32)
-                        nc.vector.tensor_scalar(
-                            out=own_term[:],
-                            in0=featT[:, c, :],
-                            scalar1=q_tab[:, c, proto : proto + 1],
-                            scalar2=None,
-                            op0=ALU.max,
-                        )
-                        terms.append(own_term)
-                    for i in range(len(terms)):
-                        add_transposed(acc[:, slot, :], terms[i][:], i == 0, i == len(terms) - 1)
+                        add_transposed(acc[:, slot, :], term[:], c == 0, c == D_CHUNKS - 1)
                 for proto in range(group * DIRECT // GROUPS, (group + 1) * DIRECT // GROUPS):
                     if proto % DIRECT_LOAD == 0:
                         q_load = direct_q.tile([P, DIRECT_LOAD, D], BF16)
@@ -428,19 +361,42 @@ def tile_prototypelearnerv4_pa_s_kernel(
                     direct(proto)
                 first_proto = DIRECT + group * BANK_CHUNKS
                 nc.vector.tensor_reduce(
-                    out=half_sums[:, first_proto : first_proto + BANK_CHUNKS],
+                    out=sums[:, first_proto : first_proto + BANK_CHUNKS],
                     in_=acc[:],
                     axis=AXIS_X,
                     op=ALU.add,
                 )
 
+            direct_sums = keep.tile([P, 1], F32)
+            nc.vector.tensor_reduce(out=direct_sums[:], in_=direct_rows[:], axis=AXIS_X, op=ALU.add)
+            proto_sums = psum_once.tile([P, P], F32, tag="feat_ps0")
+            add_transposed(proto_sums[:], direct_sums[:, 0:1].to_broadcast([P, P]), True, True)
+            nc.vector.tensor_tensor(
+                out=row_sums[:, 2:3], in0=row_sums[:, 0:1], in1=row_sums[:, 1:2], op=ALU.add
+            )
+            correction = keep.tile([P, DIRECT], F32)
+            nc.vector.tensor_scalar(
+                out=correction[:],
+                in0=proto_sums[:, 0:DIRECT],
+                scalar1=row_sums[:, 2:3],
+                scalar2=None,
+                op0=ALU.add,
+            )
+
             result = keep.tile([P, N_PROTO], F32)
             nc.vector.scalar_tensor_tensor(
-                out=result[:],
-                in0=half_sums[:],
+                out=result[:, 0:DIRECT],
+                in0=sums[:, 0:DIRECT],
                 scalar=-2.0,
                 in1=correction[:],
                 op0=ALU.mult,
                 op1=ALU.add,
+            )
+            nc.vector.tensor_scalar(
+                out=result[:, DIRECT:N_PROTO],
+                in0=sums[:, DIRECT:N_PROTO],
+                scalar1=-1.0,
+                scalar2=None,
+                op0=ALU.mult,
             )
             nc.sync.dma_start(out=out, in_=result[:])

@@ -43,7 +43,7 @@ def tile_prototypelearnerv4_pa_s_kernel(
     with (
         tc.tile_pool(name="keep", bufs=1) as keep,
         tc.tile_pool(name="stage", bufs=4) as stage,
-        tc.tile_pool(name="scalar_terms", bufs=30) as scalar_terms,
+        tc.tile_pool(name="scalar_terms", bufs=8) as scalar_terms,
         tc.tile_pool(name="direct_q", bufs=4) as direct_q,
         tc.tile_pool(name="direct_terms", bufs=2) as direct_terms,
     ):
@@ -338,16 +338,17 @@ def tile_prototypelearnerv4_pa_s_kernel(
                 acc = psum_acc.tile([P, BANK_CHUNKS, B], F32)
                 for slot in range(BANK_CHUNKS):
                     index = group * BANK_CHUNKS + slot
+                    terms = scalar_terms.tile([P, D_CHUNKS, B], F32)
                     for c in range(D_CHUNKS):
-                        term = scalar_terms.tile([P, B], F32)
                         nc.scalar.activation(
-                            out=term[:],
+                            out=terms[:, c, :],
                             in_=featT[:, c, :],
                             func=ACT.Abs,
                             bias=neg_q[:, c, index : index + 1],
                             scale=1.0,
                         )
-                        add_transposed(acc[:, slot, :], term[:], c == 0, c == D_CHUNKS - 1)
+                    for c in reversed(range(D_CHUNKS)):
+                        add_transposed(acc[:, slot, :], terms[:, c, :], c == D_CHUNKS - 1, c == 0)
                 for proto in range(group * DIRECT // GROUPS, (group + 1) * DIRECT // GROUPS):
                     if proto % DIRECT_LOAD == 0:
                         q_load = direct_q.tile([P, DIRECT_LOAD, D], BF16)

@@ -22,7 +22,7 @@ X_PASSES = D // K_PASS
 BANK_CHUNKS = 4
 
 
-DIRECT = 100
+DIRECT = 96
 DIRECT_LOAD = 4
 TURNED = N_PROTO - DIRECT
 GROUPS = TURNED // BANK_CHUNKS
@@ -61,27 +61,41 @@ def tile_prototypelearnerv4_pa_s_kernel(
         x_sb = keep.tile([P, D], BF16)
         aw_sb = keep.tile([P, D_CHUNKS, D], BF16)
 
-        nc.vector.memset(stack[:], 0.0)
-        nc.vector.memset(direct_rows[:], 0.0)
+        def load_wu3(half):
+            first = half * BANK_CHUNKS
+            nc.sync.dma_start(
+                out=wu3_sb[:, first : first + BANK_CHUNKS, :].rearrange(
+                    "m (g e) k -> m g (e k)", e=PAIR
+                ),
+                in_=pair_rows(Wu3)[:, first // PAIR : (first + BANK_CHUNKS) // PAIR, :],
+            )
+
+        def load_aw(half):
+            for g in range(half * BANK_CHUNKS // PAIR, (half + 1) * BANK_CHUNKS // PAIR):
+                nc.sync.dma_start(
+                    out=aw_sb[:, PAIR * g : PAIR * (g + 1), :].rearrange("m e k -> m (e k)"),
+                    in_=pair_rows(aW)[:, g, :],
+                )
+
         nc.sync.dma_start(out=h_up_sb[:], in_=h_up)
         nc.sync.dma_start(out=h_skip_sb[:], in_=h_skip)
-        nc.sync.dma_start(out=stack[BU2_ROW : BU2_ROW + 1, 0:F0], in_=bu2.unsqueeze(0))
-        nc.sync.dma_start(out=stack[BU3_ROW : BU3_ROW + 1, :], in_=bu3.unsqueeze(0))
-        nc.sync.dma_start(out=stack[AB_ROW : AB_ROW + 1, :], in_=ab.unsqueeze(0))
-        nc.sync.dma_start(out=stack[0:TURNED, :], in_=protos[DIRECT:N_PROTO, :])
         nc.sync.dma_start(
             out=wu2_sb[:].rearrange("m (g e) k -> m g (e k)", e=PAIR), in_=pair_rows(Wu2)
         )
-        nc.sync.dma_start(
-            out=wu3_sb[:].rearrange("m (g e) k -> m g (e k)", e=PAIR), in_=pair_rows(Wu3)
-        )
-        nc.sync.dma_start(out=x_sb[:], in_=x)
-        for g in range(D_CHUNKS // PAIR):
+        for half in range(2):
             nc.sync.dma_start(
-                out=aw_sb[:, PAIR * g : PAIR * (g + 1), :].rearrange("m e k -> m (e k)"),
-                in_=pair_rows(aW)[:, g, :],
+                out=stack[BU2_ROW : BU2_ROW + 1, half * F0 : (half + 1) * F0], in_=bu2.unsqueeze(0)
             )
-        nc.sync.dma_start(out=direct_rows[0:DIRECT, :], in_=protos[0:DIRECT, :])
+        nc.sync.dma_start(out=stack[BU3_ROW : BU3_ROW + 1, :], in_=bu3.unsqueeze(0))
+        nc.sync.dma_start(out=stack[AB_ROW : AB_ROW + 1, :], in_=ab.unsqueeze(0))
+        nc.sync.dma_start(out=stack[0:TURNED, :], in_=protos[DIRECT:N_PROTO, :])
+        nc.sync.dma_start(out=stack[TURNED + 3 : P, :], in_=protos[0 : P - TURNED - 3, :])
+        load_wu3(0)
+        nc.sync.dma_start(out=x_sb[:], in_=x)
+        load_aw(0)
+        load_wu3(1)
+        load_aw(1)
+        nc.sync.dma_start(out=direct_rows[:], in_=protos[0:P, :])
 
         z_codes = keep.tile([P, B], U32, align_bytes=64)
         z_scales = keep.tile([P, B], U8, align_bytes=64)
@@ -99,12 +113,12 @@ def tile_prototypelearnerv4_pa_s_kernel(
         x_grouped = keep.tile([P, X_PASSES, B, PACK], BF16, align_bytes=64)
 
         q_tab = keep.tile([P, D_CHUNKS, P], F32)
-        neg_q = keep.tile([P, D_CHUNKS, TURNED], F32)
         featT = keep.tile([P, D_CHUNKS, B], F32)
 
         with (
             tc.psum_pool(name="psum_t", bufs=3) as psum_t,
-            tc.psum_pool(name="psum_mx", bufs=1) as psum_mx,
+            tc.psum_pool(name="psum_mx", bufs=2) as psum_mx,
+            tc.psum_pool(name="psum_acc", bufs=3) as psum_acc,
         ):
 
             def transpose_words(src):
@@ -175,7 +189,7 @@ def tile_prototypelearnerv4_pa_s_kernel(
                 .rearrange("p g (r e) -> p g e r", e=PAIR),
             )
 
-            u2_ps = psum_mx.tile([P, F0_CHUNKS, B], F32)
+            u2_ps = psum_mx.tile([P, F0_CHUNKS, B], F32, tag="mx")
             for c in range(F0_CHUNKS):
                 nc.tensor.matmul_mx(
                     out=u2_ps[:, c, :],
@@ -199,62 +213,47 @@ def tile_prototypelearnerv4_pa_s_kernel(
             nc.vector.tensor_copy(out=u2_grouped[:], in_=u2_bf[:].rearrange("p t b -> p b t"))
             quantise(u2_grouped[:].rearrange("p b t -> p (b t)"), u2_codes[:], u2_scales[:])
 
-            nc.vector.tensor_scalar(
-                out=neg_q[:],
-                in0=q_tab[:, :, 0:TURNED],
-                scalar1=-1.0,
-                scalar2=None,
-                op0=ALU.mult,
-            )
-
-            for c in range(0, D_CHUNKS, 2):
-                to_mx_operands(
-                    c // 2,
-                    wu3_sb[:, c : c + 2, :],
-                    new_grouped(),
-                    wu3_codes[:, c : c + 2, :],
-                    wu3_scales[:, c : c + 2, :],
-                )
-            to_mx_operands(
-                0,
-                x_sb[:].rearrange("b (s k) -> b s k", s=X_PASSES),
-                x_grouped[:],
-                x_codes[:],
-                x_scales[:],
-            )
-            u3_ps = [
-                psum_mx.tile([P, BANK_CHUNKS, B], F32, name="u3_ps%d" % bank) for bank in range(2)
-            ]
-            for c in range(D_CHUNKS):
-                nc.tensor.matmul_mx(
-                    out=u3_ps[c // BANK_CHUNKS][:, c % BANK_CHUNKS, :],
-                    lhsT=wu3_codes[:, c, :].bitcast(FP8X4),
-                    lhsT_scale=wu3_scales[:, c, :],
-                    rhs=u2_codes[:].bitcast(FP8X4),
-                    rhs_scale=u2_scales[:],
-                    start=True,
-                    stop=True,
-                )
             u3_sb = keep.tile([P, D_CHUNKS, B], F32)
             rest = keep.tile([P, D_CHUNKS, B], F32)
-            for c in range(D_CHUNKS):
-                nc.scalar.activation(
-                    out=u3_sb[:, c, :],
-                    in_=u3_ps[c // BANK_CHUNKS][:, c % BANK_CHUNKS, :],
-                    func=ACT.Relu,
-                    bias=q_tab[:, c, BU3_ROW : BU3_ROW + 1],
-                    scale=1.0,
-                )
-                nc.vector.scalar_tensor_tensor(
-                    out=rest[:, c, :],
-                    in0=x_grouped[:, c // PACK, :, c % PACK],
-                    scalar=q_tab[:, c, AB_ROW : AB_ROW + 1],
-                    in1=u3_sb[:, c, :],
-                    op0=ALU.add,
-                    op1=ALU.add,
-                )
 
-            def adapter_operands(first):
+            def layer_3(first):
+                for c in range(first, first + BANK_CHUNKS, 2):
+                    to_mx_operands(
+                        c // 2,
+                        wu3_sb[:, c : c + 2, :],
+                        new_grouped(),
+                        wu3_codes[:, c : c + 2, :],
+                        wu3_scales[:, c : c + 2, :],
+                    )
+                u3_ps = psum_mx.tile([P, BANK_CHUNKS, B], F32, tag="mx")
+                for c in range(first, first + BANK_CHUNKS):
+                    nc.tensor.matmul_mx(
+                        out=u3_ps[:, c - first, :],
+                        lhsT=wu3_codes[:, c, :].bitcast(FP8X4),
+                        lhsT_scale=wu3_scales[:, c, :],
+                        rhs=u2_codes[:].bitcast(FP8X4),
+                        rhs_scale=u2_scales[:],
+                        start=True,
+                        stop=True,
+                    )
+                for c in range(first, first + BANK_CHUNKS):
+                    nc.scalar.activation(
+                        out=u3_sb[:, c, :],
+                        in_=u3_ps[:, c - first, :],
+                        func=ACT.Relu,
+                        bias=q_tab[:, c, BU3_ROW : BU3_ROW + 1],
+                        scale=1.0,
+                    )
+                    nc.vector.scalar_tensor_tensor(
+                        out=rest[:, c, :],
+                        in0=x_grouped[:, c // PACK, :, c % PACK],
+                        scalar=q_tab[:, c, AB_ROW : AB_ROW + 1],
+                        in1=u3_sb[:, c, :],
+                        op0=ALU.add,
+                        op1=ALU.add,
+                    )
+
+            def features(first):
                 for c in range(first, first + BANK_CHUNKS):
                     to_mx_operands(
                         c,
@@ -263,9 +262,7 @@ def tile_prototypelearnerv4_pa_s_kernel(
                         aw_codes[:, c, :, :],
                         aw_scales[:, c, :, :],
                     )
-
-            def features(first):
-                ad_ps = psum_mx.tile([P, BANK_CHUNKS, B], F32, name="ad_ps%d" % first)
+                ad_ps = psum_mx.tile([P, BANK_CHUNKS, B], F32, tag="mx")
                 for c in range(first, first + BANK_CHUNKS):
                     for s in range(X_PASSES):
                         nc.tensor.matmul_mx(
@@ -284,15 +281,18 @@ def tile_prototypelearnerv4_pa_s_kernel(
                     op=ALU.add,
                 )
 
-            adapter_operands(0)
+            to_mx_operands(
+                0,
+                x_sb[:].rearrange("b (s k) -> b s k", s=X_PASSES),
+                x_grouped[:],
+                x_codes[:],
+                x_scales[:],
+            )
+            layer_3(0)
             features(0)
-            adapter_operands(BANK_CHUNKS)
+            layer_3(BANK_CHUNKS)
             features(BANK_CHUNKS)
 
-        with (
-            tc.psum_pool(name="psum_once", bufs=1) as psum_once,
-            tc.psum_pool(name="psum_acc", bufs=6) as psum_acc,
-        ):
 
             def add_transposed(acc_slot, tile_in, first, last):
                 nc.tensor.matmul(
@@ -304,10 +304,15 @@ def tile_prototypelearnerv4_pa_s_kernel(
                     is_transpose=True,
                 )
 
+            direct_sums = keep.tile([P, 1], F32)
+            nc.vector.tensor_reduce(out=direct_sums[:], in_=direct_rows[:], axis=AXIS_X, op=ALU.add)
+            proto_sums = psum_acc.tile([P, P], F32, tag="acc")
+            add_transposed(proto_sums[:], direct_sums[:, 0:1].to_broadcast([P, P]), True, True)
+
             feat_rows = keep.tile([P, D], F32)
             row_sums = keep.tile([P, 3], F32)
             for half in range(2):
-                feat_ps = psum_once.tile([P, BANK_CHUNKS, P], F32, name="feat_ps%d" % half)
+                feat_ps = psum_acc.tile([P, BANK_CHUNKS, P], F32, tag="acc")
                 for i in range(BANK_CHUNKS):
                     add_transposed(feat_ps[:, i, :], featT[:, half * BANK_CHUNKS + i, :], True, True)
                 nc.scalar.activation(
@@ -318,6 +323,18 @@ def tile_prototypelearnerv4_pa_s_kernel(
                     func=ACT.Copy,
                     accum_out=row_sums[:, half : half + 1],
                 )
+
+            nc.vector.tensor_tensor(
+                out=row_sums[:, 2:3], in0=row_sums[:, 0:1], in1=row_sums[:, 1:2], op=ALU.add
+            )
+            correction = keep.tile([P, DIRECT], F32)
+            nc.vector.tensor_scalar(
+                out=correction[:],
+                in0=proto_sums[:, 0:DIRECT],
+                scalar1=row_sums[:, 2:3],
+                scalar2=None,
+                op0=ALU.add,
+            )
 
             sums = keep.tile([P, N_PROTO], F32)
 
@@ -335,7 +352,7 @@ def tile_prototypelearnerv4_pa_s_kernel(
 
             q_rows = []
             for group in range(GROUPS):
-                acc = psum_acc.tile([P, BANK_CHUNKS, B], F32)
+                acc = psum_acc.tile([P, BANK_CHUNKS, B], F32, tag="acc")
                 for slot in range(BANK_CHUNKS):
                     index = group * BANK_CHUNKS + slot
                     terms = scalar_terms.tile([P, D_CHUNKS, B], F32)
@@ -344,8 +361,8 @@ def tile_prototypelearnerv4_pa_s_kernel(
                             out=terms[:, c, :],
                             in_=featT[:, c, :],
                             func=ACT.Abs,
-                            bias=neg_q[:, c, index : index + 1],
-                            scale=1.0,
+                            bias=q_tab[:, c, index : index + 1],
+                            scale=-1.0,
                         )
                     for c in reversed(range(D_CHUNKS)):
                         add_transposed(acc[:, slot, :], terms[:, c, :], c == D_CHUNKS - 1, c == 0)
@@ -367,22 +384,6 @@ def tile_prototypelearnerv4_pa_s_kernel(
                     axis=AXIS_X,
                     op=ALU.add,
                 )
-
-            direct_sums = keep.tile([P, 1], F32)
-            nc.vector.tensor_reduce(out=direct_sums[:], in_=direct_rows[:], axis=AXIS_X, op=ALU.add)
-            proto_sums = psum_once.tile([P, P], F32, tag="feat_ps0")
-            add_transposed(proto_sums[:], direct_sums[:, 0:1].to_broadcast([P, P]), True, True)
-            nc.vector.tensor_tensor(
-                out=row_sums[:, 2:3], in0=row_sums[:, 0:1], in1=row_sums[:, 1:2], op=ALU.add
-            )
-            correction = keep.tile([P, DIRECT], F32)
-            nc.vector.tensor_scalar(
-                out=correction[:],
-                in0=proto_sums[:, 0:DIRECT],
-                scalar1=row_sums[:, 2:3],
-                scalar2=None,
-                op0=ALU.add,
-            )
 
             result = keep.tile([P, N_PROTO], F32)
             nc.vector.scalar_tensor_tensor(

@@ -22,10 +22,10 @@ X_PASSES = D // K_PASS
 BANK_CHUNKS = 4
 
 
-DIRECT = 96
+DIRECT = 94
 DIRECT_LOAD = 4
 TURNED = N_PROTO - DIRECT
-GROUPS = TURNED // BANK_CHUNKS
+GROUPS = -(-TURNED // BANK_CHUNKS)
 AB_ROW, BU3_ROW, BU2_ROW = TURNED, TURNED + 1, TURNED + 2
 
 FLOPS = 2 * B * (F1 * F0 + F0 * D + D * D) + 3 * B * N_PROTO * D
@@ -55,7 +55,6 @@ def tile_prototypelearnerv4_pa_s_kernel(
         h_up_sb = keep.tile([P, F1], BF16)
         h_skip_sb = keep.tile([P, F1], BF16)
         stack = keep.tile([P, D], BF16)
-        direct_rows = keep.tile([P, D], BF16)
         wu2_sb = keep.tile([P, F0_CHUNKS, F1], BF16)
         wu3_sb = keep.tile([P, D_CHUNKS, F0], BF16)
         x_sb = keep.tile([P, D], BF16)
@@ -95,7 +94,6 @@ def tile_prototypelearnerv4_pa_s_kernel(
         load_aw(0)
         load_wu3(1)
         load_aw(1)
-        nc.sync.dma_start(out=direct_rows[:], in_=protos[0:P, :])
 
         z_codes = keep.tile([P, B], U32, align_bytes=64)
         z_scales = keep.tile([P, B], U8, align_bytes=64)
@@ -134,10 +132,10 @@ def tile_prototypelearnerv4_pa_s_kernel(
             def quantise(grouped, codes, scales):
                 nc.vector.quantize_mx(out=codes.bitcast(FP8X4), scales=scales, in_=grouped)
 
-            def to_mx_operands(index, src, grouped, codes, scales):
+            def to_mx_operands(on_vector, src, grouped, codes, scales):
                 xt = transpose_words(src)
                 permuted = xt[:].rearrange("p s u r -> p s r u")
-                if index % 4 == 3:
+                if on_vector:
                     nc.vector.tensor_copy(out=grouped.bitcast(F32), in_=permuted)
                 else:
                     nc.scalar.copy(out=grouped.bitcast(F32), in_=permuted)
@@ -171,60 +169,62 @@ def tile_prototypelearnerv4_pa_s_kernel(
             )
             quantise(z_grouped[:].rearrange("p b t -> p (b t)"), z_codes[:], z_scales[:])
 
-            for c in range(0, F0_CHUNKS, 2):
+            def operands_wu2(c, on_vector=False):
                 to_mx_operands(
-                    c // 2,
+                    on_vector,
                     wu2_sb[:, c : c + 2, :],
                     new_grouped(),
                     wu2_codes[:, c : c + 2, :],
                     wu2_scales[:, c : c + 2, :],
                 )
 
-            stack_t = transpose_words(stack[:].rearrange("r (s k) -> r s k", s=2))
-            nc.scalar.copy(
-                out=q_tab[:].rearrange("p (g e) r -> p g e r", e=PAIR),
-                in_=stack_t[:]
-                .rearrange("p s u r -> p (s u) r")
-                .bitcast(BF16)
-                .rearrange("p g (r e) -> p g e r", e=PAIR),
-            )
+            def operands_wu3(c, on_vector=False):
+                to_mx_operands(
+                    on_vector,
+                    wu3_sb[:, c : c + 2, :],
+                    new_grouped(),
+                    wu3_codes[:, c : c + 2, :],
+                    wu3_scales[:, c : c + 2, :],
+                )
 
-            u2_ps = psum_mx.tile([P, F0_CHUNKS, B], F32, tag="mx")
-            for c in range(F0_CHUNKS):
-                nc.tensor.matmul_mx(
-                    out=u2_ps[:, c, :],
-                    lhsT=wu2_codes[:, c, :].bitcast(FP8X4),
-                    lhsT_scale=wu2_scales[:, c, :],
-                    rhs=z_codes[:].bitcast(FP8X4),
-                    rhs_scale=z_scales[:],
-                    start=True,
-                    stop=True,
+            def operands_aw(c, on_vector=False):
+                to_mx_operands(
+                    on_vector,
+                    aw_sb[:, c, :].rearrange("m (s k) -> m s k", s=X_PASSES),
+                    new_grouped(),
+                    aw_codes[:, c, :, :],
+                    aw_scales[:, c, :, :],
                 )
-            u2_bf = keep.tile([P, F0_CHUNKS, B], BF16)
-            for c in range(F0_CHUNKS):
-                nc.scalar.activation(
-                    out=u2_bf[:, c, :],
-                    in_=u2_ps[:, c, :],
-                    func=ACT.Relu,
-                    bias=q_tab[:, c, BU2_ROW : BU2_ROW + 1],
-                    scale=1.0,
-                )
-            u2_grouped = keep.tile([P, B, PACK], BF16, align_bytes=64)
-            nc.vector.tensor_copy(out=u2_grouped[:], in_=u2_bf[:].rearrange("p t b -> p b t"))
-            quantise(u2_grouped[:].rearrange("p b t -> p (b t)"), u2_codes[:], u2_scales[:])
+
+            def layer_2():
+                u2_ps = psum_mx.tile([P, F0_CHUNKS, B], F32, tag="mx")
+                for c in range(F0_CHUNKS):
+                    nc.tensor.matmul_mx(
+                        out=u2_ps[:, c, :],
+                        lhsT=wu2_codes[:, c, :].bitcast(FP8X4),
+                        lhsT_scale=wu2_scales[:, c, :],
+                        rhs=z_codes[:].bitcast(FP8X4),
+                        rhs_scale=z_scales[:],
+                        start=True,
+                        stop=True,
+                    )
+                u2_bf = keep.tile([P, F0_CHUNKS, B], BF16)
+                for c in range(F0_CHUNKS):
+                    nc.scalar.activation(
+                        out=u2_bf[:, c, :],
+                        in_=u2_ps[:, c, :],
+                        func=ACT.Relu,
+                        bias=q_tab[:, c, BU2_ROW : BU2_ROW + 1],
+                        scale=1.0,
+                    )
+                u2_grouped = keep.tile([P, B, PACK], BF16, align_bytes=64)
+                nc.vector.tensor_copy(out=u2_grouped[:], in_=u2_bf[:].rearrange("p t b -> p b t"))
+                quantise(u2_grouped[:].rearrange("p b t -> p (b t)"), u2_codes[:], u2_scales[:])
 
             u3_sb = keep.tile([P, D_CHUNKS, B], F32)
             rest = keep.tile([P, D_CHUNKS, B], F32)
 
             def layer_3(first):
-                for c in range(first, first + BANK_CHUNKS, 2):
-                    to_mx_operands(
-                        c // 2,
-                        wu3_sb[:, c : c + 2, :],
-                        new_grouped(),
-                        wu3_codes[:, c : c + 2, :],
-                        wu3_scales[:, c : c + 2, :],
-                    )
                 u3_ps = psum_mx.tile([P, BANK_CHUNKS, B], F32, tag="mx")
                 for c in range(first, first + BANK_CHUNKS):
                     nc.tensor.matmul_mx(
@@ -254,14 +254,6 @@ def tile_prototypelearnerv4_pa_s_kernel(
                     )
 
             def features(first):
-                for c in range(first, first + BANK_CHUNKS):
-                    to_mx_operands(
-                        c,
-                        aw_sb[:, c, :].rearrange("m (s k) -> m s k", s=X_PASSES),
-                        new_grouped(),
-                        aw_codes[:, c, :, :],
-                        aw_scales[:, c, :, :],
-                    )
                 ad_ps = psum_mx.tile([P, BANK_CHUNKS, B], F32, tag="mx")
                 for c in range(first, first + BANK_CHUNKS):
                     for s in range(X_PASSES):
@@ -281,17 +273,43 @@ def tile_prototypelearnerv4_pa_s_kernel(
                     op=ALU.add,
                 )
 
-            to_mx_operands(
-                0,
-                x_sb[:].rearrange("b (s k) -> b s k", s=X_PASSES),
-                x_grouped[:],
-                x_codes[:],
-                x_scales[:],
-            )
-            layer_3(0)
-            features(0)
-            layer_3(BANK_CHUNKS)
-            features(BANK_CHUNKS)
+            with tc.manual_schedule(engines={mybir.EngineType.PE}):
+                operands_wu2(0)
+                operands_wu2(2)
+
+                stack_t = transpose_words(stack[:].rearrange("r (s k) -> r s k", s=2))
+                nc.scalar.copy(
+                    out=q_tab[:].rearrange("p (g e) r -> p g e r", e=PAIR),
+                    in_=stack_t[:]
+                    .rearrange("p s u r -> p (s u) r")
+                    .bitcast(BF16)
+                    .rearrange("p g (r e) -> p g e r", e=PAIR),
+                )
+
+                operands_wu3(0, on_vector=True)
+                operands_wu3(2)
+                layer_2()
+                to_mx_operands(
+                    False,
+                    x_sb[:].rearrange("b (s k) -> b s k", s=X_PASSES),
+                    x_grouped[:],
+                    x_codes[:],
+                    x_scales[:],
+                )
+                operands_aw(0)
+                operands_aw(1, on_vector=True)
+                layer_3(0)
+                operands_aw(2)
+                operands_aw(3)
+                operands_wu3(4)
+                operands_wu3(6, on_vector=True)
+                features(0)
+                operands_aw(4)
+                operands_aw(5)
+                operands_aw(6)
+                layer_3(BANK_CHUNKS)
+                operands_aw(7, on_vector=True)
+                features(BANK_CHUNKS)
 
 
             def add_transposed(acc_slot, tile_in, first, last):
@@ -304,37 +322,29 @@ def tile_prototypelearnerv4_pa_s_kernel(
                     is_transpose=True,
                 )
 
-            direct_sums = keep.tile([P, 1], F32)
-            nc.vector.tensor_reduce(out=direct_sums[:], in_=direct_rows[:], axis=AXIS_X, op=ALU.add)
-            proto_sums = psum_acc.tile([P, P], F32, tag="acc")
-            add_transposed(proto_sums[:], direct_sums[:, 0:1].to_broadcast([P, P]), True, True)
-
             feat_rows = keep.tile([P, D], F32)
             row_sums = keep.tile([P, 3], F32)
             for half in range(2):
                 feat_ps = psum_acc.tile([P, BANK_CHUNKS, P], F32, tag="acc")
                 for i in range(BANK_CHUNKS):
                     add_transposed(feat_ps[:, i, :], featT[:, half * BANK_CHUNKS + i, :], True, True)
-                nc.scalar.activation(
-                    out=feat_rows[:, half * (D // 2) : (half + 1) * (D // 2)].rearrange(
-                        "b (g p e) -> b g p e", g=BANK_CHUNKS // PAIR, e=PAIR
-                    ),
-                    in_=feat_ps[:].rearrange("b (g e) p -> b g p e", e=PAIR),
-                    func=ACT.Copy,
-                    accum_out=row_sums[:, half : half + 1],
+                rows = feat_rows[:, half * (D // 2) : (half + 1) * (D // 2)].rearrange(
+                    "b (g p e) -> b g p e", g=BANK_CHUNKS // PAIR, e=PAIR
                 )
-
-            nc.vector.tensor_tensor(
-                out=row_sums[:, 2:3], in0=row_sums[:, 0:1], in1=row_sums[:, 1:2], op=ALU.add
-            )
-            correction = keep.tile([P, DIRECT], F32)
-            nc.vector.tensor_scalar(
-                out=correction[:],
-                in0=proto_sums[:, 0:DIRECT],
-                scalar1=row_sums[:, 2:3],
-                scalar2=None,
-                op0=ALU.add,
-            )
+                turned = feat_ps[:].rearrange("b (g e) p -> b g p e", e=PAIR)
+                half_sum = row_sums[:, half : half + 1]
+                if half == 0:
+                    nc.scalar.activation(out=rows, in_=turned, func=ACT.Copy, accum_out=half_sum)
+                else:
+                    nc.vector.tensor_scalar(
+                        out=rows,
+                        in0=turned,
+                        scalar1=1.0,
+                        scalar2=None,
+                        op0=ALU.mult,
+                        op1=ALU.add,
+                        accum_out=half_sum,
+                    )
 
             sums = keep.tile([P, N_PROTO], F32)
 
@@ -350,10 +360,23 @@ def tile_prototypelearnerv4_pa_s_kernel(
                     accum_out=sums[:, proto : proto + 1],
                 )
 
+            direct_rows = keep.tile([P, D], BF16)
+            copied_rows = keep.tile([P, D], BF16)
+            direct_sums = keep.tile([P, 1], F32)
+
             q_rows = []
             for group in range(GROUPS):
+                if group == GROUPS // 2:
+                    nc.sync.dma_start(out=direct_rows[:], in_=protos[0:P, :])
+                    nc.scalar.activation(
+                        out=copied_rows[:],
+                        in_=direct_rows[:],
+                        func=ACT.Copy,
+                        accum_out=direct_sums[:],
+                    )
                 acc = psum_acc.tile([P, BANK_CHUNKS, B], F32, tag="acc")
-                for slot in range(BANK_CHUNKS):
+                slots = min(BANK_CHUNKS, TURNED - group * BANK_CHUNKS)
+                for slot in range(slots):
                     index = group * BANK_CHUNKS + slot
                     terms = scalar_terms.tile([P, D_CHUNKS, B], F32)
                     for c in range(D_CHUNKS):
@@ -369,9 +392,10 @@ def tile_prototypelearnerv4_pa_s_kernel(
                 for proto in range(group * DIRECT // GROUPS, (group + 1) * DIRECT // GROUPS):
                     if proto % DIRECT_LOAD == 0:
                         q_load = direct_q.tile([P, DIRECT_LOAD, D], BF16)
+                        count = min(DIRECT_LOAD, DIRECT - proto)
                         nc.sync.dma_start(
-                            out=q_load[:].rearrange("b r d -> b (r d)"),
-                            in_=protos[proto : proto + DIRECT_LOAD, :]
+                            out=q_load[:, 0:count, :].rearrange("b r d -> b (r d)"),
+                            in_=protos[proto : proto + count, :]
                             .rearrange("r d -> (r d)")
                             .partition_broadcast(P),
                         )
@@ -379,11 +403,25 @@ def tile_prototypelearnerv4_pa_s_kernel(
                     direct(proto)
                 first_proto = DIRECT + group * BANK_CHUNKS
                 nc.vector.tensor_reduce(
-                    out=sums[:, first_proto : first_proto + BANK_CHUNKS],
-                    in_=acc[:],
+                    out=sums[:, first_proto : first_proto + slots],
+                    in_=acc[:, 0:slots, :],
                     axis=AXIS_X,
                     op=ALU.add,
                 )
+
+            proto_sums = psum_acc.tile([P, P], F32, tag="acc")
+            add_transposed(proto_sums[:], direct_sums[:, 0:1].to_broadcast([P, P]), True, True)
+            nc.vector.tensor_tensor(
+                out=row_sums[:, 2:3], in0=row_sums[:, 0:1], in1=row_sums[:, 1:2], op=ALU.add
+            )
+            correction = keep.tile([P, DIRECT], F32)
+            nc.vector.tensor_scalar(
+                out=correction[:],
+                in0=proto_sums[:, 0:DIRECT],
+                scalar1=row_sums[:, 2:3],
+                scalar2=None,
+                op0=ALU.add,
+            )
 
             result = keep.tile([P, N_PROTO], F32)
             nc.vector.scalar_tensor_tensor(

@@ -22,11 +22,14 @@ X_PASSES = D // K_PASS
 BANK_CHUNKS = 4
 
 
-DIRECT = 94
+DIRECT = 96
 DIRECT_LOAD = 4
 TURNED = N_PROTO - DIRECT
 GROUPS = -(-TURNED // BANK_CHUNKS)
-AB_ROW, BU3_ROW, BU2_ROW = TURNED, TURNED + 1, TURNED + 2
+AB_ROW, BU3_ROW, BU2_ROW = 0, 1, 2
+STACKED_ROW = 16
+STACKED = P - STACKED_ROW
+TURNED_ROW = P - TURNED
 
 FLOPS = 2 * B * (F1 * F0 + F0 * D + D * D) + 3 * B * N_PROTO * D
 
@@ -47,6 +50,9 @@ def tile_prototypelearnerv4_pa_s_kernel(
         tc.tile_pool(name="direct_q", bufs=4) as direct_q,
         tc.tile_pool(name="direct_terms", bufs=2) as direct_terms,
     ):
+        stack = keep.tile([P, D], BF16)
+        nc.gpsimd.memset(stack[0:STACKED_ROW, :], 0.0)
+
         ident_bf = keep.tile([P, P], BF16)
         make_identity(nc, ident_bf[:])
         ident_f32 = keep.tile([P, P], F32)
@@ -54,7 +60,6 @@ def tile_prototypelearnerv4_pa_s_kernel(
 
         h_up_sb = keep.tile([P, F1], BF16)
         h_skip_sb = keep.tile([P, F1], BF16)
-        stack = keep.tile([P, D], BF16)
         wu2_sb = keep.tile([P, F0_CHUNKS, F1], BF16)
         wu3_sb = keep.tile([P, D_CHUNKS, F0], BF16)
         x_sb = keep.tile([P, D], BF16)
@@ -81,14 +86,10 @@ def tile_prototypelearnerv4_pa_s_kernel(
         nc.sync.dma_start(
             out=wu2_sb[:].rearrange("m (g e) k -> m g (e k)", e=PAIR), in_=pair_rows(Wu2)
         )
-        for half in range(2):
-            nc.sync.dma_start(
-                out=stack[BU2_ROW : BU2_ROW + 1, half * F0 : (half + 1) * F0], in_=bu2.unsqueeze(0)
-            )
+        nc.sync.dma_start(out=stack[BU2_ROW : BU2_ROW + 1, 0:F0], in_=bu2.unsqueeze(0))
         nc.sync.dma_start(out=stack[BU3_ROW : BU3_ROW + 1, :], in_=bu3.unsqueeze(0))
         nc.sync.dma_start(out=stack[AB_ROW : AB_ROW + 1, :], in_=ab.unsqueeze(0))
-        nc.sync.dma_start(out=stack[0:TURNED, :], in_=protos[DIRECT:N_PROTO, :])
-        nc.sync.dma_start(out=stack[TURNED + 3 : P, :], in_=protos[0 : P - TURNED - 3, :])
+        nc.sync.dma_start(out=stack[STACKED_ROW:P, :], in_=protos[N_PROTO - STACKED : N_PROTO, :])
         load_wu3(0)
         nc.sync.dma_start(out=x_sb[:], in_=x)
         load_aw(0)
@@ -384,7 +385,7 @@ def tile_prototypelearnerv4_pa_s_kernel(
                             out=terms[:, c, :],
                             in_=featT[:, c, :],
                             func=ACT.Abs,
-                            bias=q_tab[:, c, index : index + 1],
+                            bias=q_tab[:, c, TURNED_ROW + index : TURNED_ROW + index + 1],
                             scale=-1.0,
                         )
                     for c in reversed(range(D_CHUNKS)):

import concourse.mybir as mybir
from concourse.masks import make_identity

F32 = mybir.dt.float32
BF16 = mybir.dt.bfloat16
U32 = mybir.dt.uint32
U8 = mybir.dt.uint8
FP8X4 = mybir.dt.float8_e4m3fn_x4
ALU = mybir.AluOpType
ACT = mybir.ActivationFunctionType
AXIS_X = mybir.AxisListType.X

P = 128
PACK = 4
K_PASS = P * PACK
PAIR = 2

B, D, F0, F1, N_PROTO = 128, 1024, 512, 512, 200
D_CHUNKS = D // P
F0_CHUNKS = F0 // P
X_PASSES = D // K_PASS
BANK_CHUNKS = 4


DIRECT = 96
DIRECT_LOAD = 4
TURNED = N_PROTO - DIRECT
GROUPS = -(-TURNED // BANK_CHUNKS)
AB_ROW, BU3_ROW, BU2_ROW = 0, 1, 2
STACKED_ROW = 16
STACKED = P - STACKED_ROW
TURNED_ROW = P - TURNED

FLOPS = 2 * B * (F1 * F0 + F0 * D + D * D) + 3 * B * N_PROTO * D


def pair_rows(w):
    return w.rearrange("(g m e) k -> m g (e k)", m=P, e=PAIR)


def tile_prototypelearnerv4_pa_s_kernel(
    tc, x, aW, ab, h_up, h_skip, Wu2, bu2, Wu3, bu3, protos, out
):
    nc = tc.nc

    with (
        tc.tile_pool(name="keep", bufs=1) as keep,
        tc.tile_pool(name="stage", bufs=4) as stage,
        tc.tile_pool(name="scalar_terms", bufs=8) as scalar_terms,
        tc.tile_pool(name="direct_q", bufs=4) as direct_q,
        tc.tile_pool(name="direct_terms", bufs=2) as direct_terms,
    ):
        stack = keep.tile([P, D], BF16)
        nc.gpsimd.memset(stack[0:STACKED_ROW, :], 0.0)

        ident_bf = keep.tile([P, P], BF16)
        make_identity(nc, ident_bf[:])
        ident_f32 = keep.tile([P, P], F32)
        make_identity(nc, ident_f32[:])

        h_up_sb = keep.tile([P, F1], BF16)
        h_skip_sb = keep.tile([P, F1], BF16)
        wu2_sb = keep.tile([P, F0_CHUNKS, F1], BF16)
        wu3_sb = keep.tile([P, D_CHUNKS, F0], BF16)
        x_sb = keep.tile([P, D], BF16)
        aw_sb = keep.tile([P, D_CHUNKS, D], BF16)

        def load_wu3(half):
            first = half * BANK_CHUNKS
            nc.sync.dma_start(
                out=wu3_sb[:, first : first + BANK_CHUNKS, :].rearrange(
                    "m (g e) k -> m g (e k)", e=PAIR
                ),
                in_=pair_rows(Wu3)[:, first // PAIR : (first + BANK_CHUNKS) // PAIR, :],
            )

        def load_aw(half):
            for g in range(half * BANK_CHUNKS // PAIR, (half + 1) * BANK_CHUNKS // PAIR):
                nc.sync.dma_start(
                    out=aw_sb[:, PAIR * g : PAIR * (g + 1), :].rearrange("m e k -> m (e k)"),
                    in_=pair_rows(aW)[:, g, :],
                )

        nc.sync.dma_start(out=h_up_sb[:], in_=h_up)
        nc.sync.dma_start(out=h_skip_sb[:], in_=h_skip)
        nc.sync.dma_start(
            out=wu2_sb[:].rearrange("m (g e) k -> m g (e k)", e=PAIR), in_=pair_rows(Wu2)
        )
        nc.sync.dma_start(out=stack[BU2_ROW : BU2_ROW + 1, 0:F0], in_=bu2.unsqueeze(0))
        nc.sync.dma_start(out=stack[BU3_ROW : BU3_ROW + 1, :], in_=bu3.unsqueeze(0))
        nc.sync.dma_start(out=stack[AB_ROW : AB_ROW + 1, :], in_=ab.unsqueeze(0))
        nc.sync.dma_start(out=stack[STACKED_ROW:P, :], in_=protos[N_PROTO - STACKED : N_PROTO, :])
        load_wu3(0)
        nc.sync.dma_start(out=x_sb[:], in_=x)
        load_aw(0)
        load_wu3(1)
        load_aw(1)

        z_codes = keep.tile([P, B], U32, align_bytes=64)
        z_scales = keep.tile([P, B], U8, align_bytes=64)
        u2_codes = keep.tile([P, B], U32, align_bytes=64)
        u2_scales = keep.tile([P, B], U8, align_bytes=64)
        x_codes = keep.tile([P, X_PASSES, B], U32, align_bytes=64)
        x_scales = keep.tile([P, X_PASSES, B], U8, align_bytes=64)
        wu2_codes = keep.tile([P, F0_CHUNKS, P], U32, align_bytes=64)
        wu2_scales = keep.tile([P, F0_CHUNKS, P], U8, align_bytes=64)
        wu3_codes = keep.tile([P, D_CHUNKS, P], U32, align_bytes=64)
        wu3_scales = keep.tile([P, D_CHUNKS, P], U8, align_bytes=64)
        aw_codes = keep.tile([P, D_CHUNKS, X_PASSES, P], U32, align_bytes=64)
        aw_scales = keep.tile([P, D_CHUNKS, X_PASSES, P], U8, align_bytes=64)

        x_grouped = keep.tile([P, X_PASSES, B, PACK], BF16, align_bytes=64)

        q_tab = keep.tile([P, D_CHUNKS, P], F32)
        featT = keep.tile([P, D_CHUNKS, B], F32)

        with (
            tc.psum_pool(name="psum_t", bufs=3) as psum_t,
            tc.psum_pool(name="psum_mx", bufs=2) as psum_mx,
            tc.psum_pool(name="psum_acc", bufs=3) as psum_acc,
        ):

            def transpose_words(src):
                words = src.bitcast(F32)
                xt = psum_t.tile([P, 2, PAIR, P], F32, tag="xt")
                for s in range(2):
                    for u in range(PAIR):
                        nc.tensor.transpose(
                            xt[:, s, u, :], words[:, s, u * P : (u + 1) * P], ident_f32[:]
                        )
                return xt

            def quantise(grouped, codes, scales):
                nc.vector.quantize_mx(out=codes.bitcast(FP8X4), scales=scales, in_=grouped)

            def to_mx_operands(on_vector, src, grouped, codes, scales):
                xt = transpose_words(src)
                permuted = xt[:].rearrange("p s u r -> p s r u")
                if on_vector:
                    nc.vector.tensor_copy(out=grouped.bitcast(F32), in_=permuted)
                else:
                    nc.scalar.copy(out=grouped.bitcast(F32), in_=permuted)
                quantise(
                    grouped.rearrange("p s r t -> p (s r t)"),
                    codes.rearrange("p s r -> p (s r)"),
                    scales.rearrange("p s r -> p (s r)"),
                )

            def new_grouped():
                grouped = stage.tile([P, 2, P, PACK], BF16, align_bytes=64)
                return grouped[:]

            z_sorted = keep.tile([P, PAIR, F1 // PAIR], BF16)
            nc.vector.tensor_tensor(
                out=z_sorted[:],
                in0=h_up_sb[:].rearrange("b (w e) -> b e w", e=PAIR),
                in1=h_skip_sb[:].rearrange("b (w e) -> b e w", e=PAIR),
                op=ALU.add,
            )
            zt = psum_t.tile([P, PAIR, PAIR, B], BF16, tag="xt")
            for u in range(PAIR):
                for e in range(PAIR):
                    nc.tensor.transpose(
                        zt[:, u, e, :], z_sorted[:, e, u * P : (u + 1) * P], ident_bf[:]
                    )
            z_grouped = keep.tile([P, B, PACK], BF16, align_bytes=64)
            nc.scalar.copy(
                out=z_grouped[:],
                in_=zt[:].rearrange("p u e b -> p (u e) b").rearrange("p t b -> p b t"),
            )
            quantise(z_grouped[:].rearrange("p b t -> p (b t)"), z_codes[:], z_scales[:])

            def operands_wu2(c, on_vector=False):
                to_mx_operands(
                    on_vector,
                    wu2_sb[:, c : c + 2, :],
                    new_grouped(),
                    wu2_codes[:, c : c + 2, :],
                    wu2_scales[:, c : c + 2, :],
                )

            def operands_wu3(c, on_vector=False):
                to_mx_operands(
                    on_vector,
                    wu3_sb[:, c : c + 2, :],
                    new_grouped(),
                    wu3_codes[:, c : c + 2, :],
                    wu3_scales[:, c : c + 2, :],
                )

            def operands_aw(c, on_vector=False):
                to_mx_operands(
                    on_vector,
                    aw_sb[:, c, :].rearrange("m (s k) -> m s k", s=X_PASSES),
                    new_grouped(),
                    aw_codes[:, c, :, :],
                    aw_scales[:, c, :, :],
                )

            def layer_2():
                u2_ps = psum_mx.tile([P, F0_CHUNKS, B], F32, tag="mx")
                for c in range(F0_CHUNKS):
                    nc.tensor.matmul_mx(
                        out=u2_ps[:, c, :],
                        lhsT=wu2_codes[:, c, :].bitcast(FP8X4),
                        lhsT_scale=wu2_scales[:, c, :],
                        rhs=z_codes[:].bitcast(FP8X4),
                        rhs_scale=z_scales[:],
                        start=True,
                        stop=True,
                    )
                u2_bf = keep.tile([P, F0_CHUNKS, B], BF16)
                for c in range(F0_CHUNKS):
                    nc.scalar.activation(
                        out=u2_bf[:, c, :],
                        in_=u2_ps[:, c, :],
                        func=ACT.Relu,
                        bias=q_tab[:, c, BU2_ROW : BU2_ROW + 1],
                        scale=1.0,
                    )
                u2_grouped = keep.tile([P, B, PACK], BF16, align_bytes=64)
                nc.vector.tensor_copy(out=u2_grouped[:], in_=u2_bf[:].rearrange("p t b -> p b t"))
                quantise(u2_grouped[:].rearrange("p b t -> p (b t)"), u2_codes[:], u2_scales[:])

            u3_sb = keep.tile([P, D_CHUNKS, B], F32)
            rest = keep.tile([P, D_CHUNKS, B], F32)

            def layer_3(first):
                u3_ps = psum_mx.tile([P, BANK_CHUNKS, B], F32, tag="mx")
                for c in range(first, first + BANK_CHUNKS):
                    nc.tensor.matmul_mx(
                        out=u3_ps[:, c - first, :],
                        lhsT=wu3_codes[:, c, :].bitcast(FP8X4),
                        lhsT_scale=wu3_scales[:, c, :],
                        rhs=u2_codes[:].bitcast(FP8X4),
                        rhs_scale=u2_scales[:],
                        start=True,
                        stop=True,
                    )
                for c in range(first, first + BANK_CHUNKS):
                    nc.scalar.activation(
                        out=u3_sb[:, c, :],
                        in_=u3_ps[:, c - first, :],
                        func=ACT.Relu,
                        bias=q_tab[:, c, BU3_ROW : BU3_ROW + 1],
                        scale=1.0,
                    )
                    nc.vector.scalar_tensor_tensor(
                        out=rest[:, c, :],
                        in0=x_grouped[:, c // PACK, :, c % PACK],
                        scalar=q_tab[:, c, AB_ROW : AB_ROW + 1],
                        in1=u3_sb[:, c, :],
                        op0=ALU.add,
                        op1=ALU.add,
                    )

            def features(first):
                ad_ps = psum_mx.tile([P, BANK_CHUNKS, B], F32, tag="mx")
                for c in range(first, first + BANK_CHUNKS):
                    for s in range(X_PASSES):
                        nc.tensor.matmul_mx(
                            out=ad_ps[:, c - first, :],
                            lhsT=aw_codes[:, c, s, :].bitcast(FP8X4),
                            lhsT_scale=aw_scales[:, c, s, :],
                            rhs=x_codes[:, s, :].bitcast(FP8X4),
                            rhs_scale=x_scales[:, s, :],
                            start=(s == 0),
                            stop=(s == X_PASSES - 1),
                        )
                nc.vector.tensor_tensor(
                    out=featT[:, first : first + BANK_CHUNKS, :],
                    in0=ad_ps[:],
                    in1=rest[:, first : first + BANK_CHUNKS, :],
                    op=ALU.add,
                )

            with tc.manual_schedule(engines={mybir.EngineType.PE}):
                operands_wu2(0)
                operands_wu2(2)

                stack_t = transpose_words(stack[:].rearrange("r (s k) -> r s k", s=2))
                nc.scalar.copy(
                    out=q_tab[:].rearrange("p (g e) r -> p g e r", e=PAIR),
                    in_=stack_t[:]
                    .rearrange("p s u r -> p (s u) r")
                    .bitcast(BF16)
                    .rearrange("p g (r e) -> p g e r", e=PAIR),
                )

                operands_wu3(0, on_vector=True)
                operands_wu3(2)
                layer_2()
                to_mx_operands(
                    False,
                    x_sb[:].rearrange("b (s k) -> b s k", s=X_PASSES),
                    x_grouped[:],
                    x_codes[:],
                    x_scales[:],
                )
                operands_aw(0)
                operands_aw(1, on_vector=True)
                layer_3(0)
                operands_aw(2)
                operands_aw(3)
                operands_wu3(4)
                operands_wu3(6, on_vector=True)
                features(0)
                operands_aw(4)
                operands_aw(5)
                operands_aw(6)
                layer_3(BANK_CHUNKS)
                operands_aw(7, on_vector=True)
                features(BANK_CHUNKS)


            def add_transposed(acc_slot, tile_in, first, last):
                nc.tensor.matmul(
                    out=acc_slot,
                    lhsT=tile_in,
                    rhs=ident_f32[:],
                    start=first,
                    stop=last,
                    is_transpose=True,
                )

            feat_rows = keep.tile([P, D], F32)
            row_sums = keep.tile([P, 3], F32)
            for half in range(2):
                feat_ps = psum_acc.tile([P, BANK_CHUNKS, P], F32, tag="acc")
                for i in range(BANK_CHUNKS):
                    add_transposed(feat_ps[:, i, :], featT[:, half * BANK_CHUNKS + i, :], True, True)
                rows = feat_rows[:, half * (D // 2) : (half + 1) * (D // 2)].rearrange(
                    "b (g p e) -> b g p e", g=BANK_CHUNKS // PAIR, e=PAIR
                )
                turned = feat_ps[:].rearrange("b (g e) p -> b g p e", e=PAIR)
                half_sum = row_sums[:, half : half + 1]
                if half == 0:
                    nc.scalar.activation(out=rows, in_=turned, func=ACT.Copy, accum_out=half_sum)
                else:
                    nc.vector.tensor_scalar(
                        out=rows,
                        in0=turned,
                        scalar1=1.0,
                        scalar2=None,
                        op0=ALU.mult,
                        op1=ALU.add,
                        accum_out=half_sum,
                    )

            sums = keep.tile([P, N_PROTO], F32)

            def direct(proto):
                junk = direct_terms.tile([P, D], F32)
                nc.vector.scalar_tensor_tensor(
                    out=junk[:],
                    in0=q_rows[proto // DIRECT_LOAD][:, proto % DIRECT_LOAD, :],
                    scalar=1.0,
                    in1=feat_rows[:],
                    op0=ALU.mult,
                    op1=ALU.max,
                    accum_out=sums[:, proto : proto + 1],
                )

            direct_rows = keep.tile([P, D], BF16)
            copied_rows = keep.tile([P, D], BF16)
            direct_sums = keep.tile([P, 1], F32)

            q_rows = []
            for group in range(GROUPS):
                if group == GROUPS // 2:
                    nc.sync.dma_start(out=direct_rows[:], in_=protos[0:P, :])
                    nc.scalar.activation(
                        out=copied_rows[:],
                        in_=direct_rows[:],
                        func=ACT.Copy,
                        accum_out=direct_sums[:],
                    )
                acc = psum_acc.tile([P, BANK_CHUNKS, B], F32, tag="acc")
                slots = min(BANK_CHUNKS, TURNED - group * BANK_CHUNKS)
                for slot in range(slots):
                    index = group * BANK_CHUNKS + slot
                    terms = scalar_terms.tile([P, D_CHUNKS, B], F32)
                    for c in range(D_CHUNKS):
                        nc.scalar.activation(
                            out=terms[:, c, :],
                            in_=featT[:, c, :],
                            func=ACT.Abs,
                            bias=q_tab[:, c, TURNED_ROW + index : TURNED_ROW + index + 1],
                            scale=-1.0,
                        )
                    for c in reversed(range(D_CHUNKS)):
                        add_transposed(acc[:, slot, :], terms[:, c, :], c == D_CHUNKS - 1, c == 0)
                for proto in range(group * DIRECT // GROUPS, (group + 1) * DIRECT // GROUPS):
                    if proto % DIRECT_LOAD == 0:
                        q_load = direct_q.tile([P, DIRECT_LOAD, D], BF16)
                        count = min(DIRECT_LOAD, DIRECT - proto)
                        nc.sync.dma_start(
                            out=q_load[:, 0:count, :].rearrange("b r d -> b (r d)"),
                            in_=protos[proto : proto + count, :]
                            .rearrange("r d -> (r d)")
                            .partition_broadcast(P),
                        )
                        q_rows.append(q_load)
                    direct(proto)
                first_proto = DIRECT + group * BANK_CHUNKS
                nc.vector.tensor_reduce(
                    out=sums[:, first_proto : first_proto + slots],
                    in_=acc[:, 0:slots, :],
                    axis=AXIS_X,
                    op=ALU.add,
                )

            proto_sums = psum_acc.tile([P, P], F32, tag="acc")
            add_transposed(proto_sums[:], direct_sums[:, 0:1].to_broadcast([P, P]), True, True)
            nc.vector.tensor_tensor(
                out=row_sums[:, 2:3], in0=row_sums[:, 0:1], in1=row_sums[:, 1:2], op=ALU.add
            )
            correction = keep.tile([P, DIRECT], F32)
            nc.vector.tensor_scalar(
                out=correction[:],
                in0=proto_sums[:, 0:DIRECT],
                scalar1=row_sums[:, 2:3],
                scalar2=None,
                op0=ALU.add,
            )

            result = keep.tile([P, N_PROTO], F32)
            nc.vector.scalar_tensor_tensor(
                out=result[:, 0:DIRECT],
                in0=sums[:, 0:DIRECT],
                scalar=-2.0,
                in1=correction[:],
                op0=ALU.mult,
                op1=ALU.add,
            )
            nc.vector.tensor_scalar(
                out=result[:, DIRECT:N_PROTO],
                in0=sums[:, DIRECT:N_PROTO],
                scalar1=-1.0,
                scalar2=None,
                op0=ALU.mult,
            )
            nc.sync.dma_start(out=out, in_=result[:])
